import numpy as np
import ml_dtypes


def mxq(x, axis, fmt="e4m3"):
    dtype, down = {"e4m3": (ml_dtypes.float8_e4m3fn, 7), "e5m2": (ml_dtypes.float8_e5m2, 14)}[fmt]
    v = np.moveaxis(np.asarray(x, np.float32).astype(ml_dtypes.bfloat16).astype(np.float64), axis, -1)
    blocks = v.reshape(v.shape[:-1] + (-1, 32))
    amax = np.abs(blocks).max(-1, keepdims=True)
    byte = np.maximum(np.where(amax > 0, np.frexp(amax)[1] - 1 + 127, 0) - down, 1)
    scale = np.exp2(byte - 127.0)
    codes = (blocks / scale).astype(np.float32).astype(dtype).astype(np.float64)
    return np.moveaxis((codes * scale).reshape(v.shape), -1, axis)


WIDE = False


def mx_kscale(k):
    if not WIDE:
        return np.ones(k)
    levels = np.array([10, -10, 5, -5, 0])
    a = np.random.permutation(np.resize(levels, k // 512 * 4)).reshape(k // 512, 4)
    idx = np.arange(k)
    return np.exp2(a[idx // 512, idx % 128 // 32])


BF16 = ml_dtypes.bfloat16


def bf(x):
    return np.asarray(x, np.float32).astype(BF16)


def f64(x):
    return np.asarray(x).astype(np.float64)


E2M1 = np.array([0.0, 0.5, 1.0, 1.5, 2.0, 3.0, 4.0, 6.0, -0.0, -0.5, -1.0, -1.5, -2.0, -3.0, -4.0, -6.0])


def pack_weight(w, fmt):
    k, n = w.shape
    w = f64(bf(w)).reshape(k // 32, 32, n)
    amax = np.abs(w).max(1)
    if fmt == "e4m3":
        byte = np.frexp(amax)[1] - 1 + 127 - 7
    else:
        mant, ex = np.frexp(amax / 6.0)
        byte = np.where(mant > 0.5, ex, ex - 1) + 127
    byte = np.clip(np.where(amax > 0, byte, 1), 1, 254)
    scaled = (w * np.exp2(127.0 - byte)[:, None, :]).reshape(k, n).astype(np.float32)
    by_word = np.ascontiguousarray(scaled.reshape(k // 512, 128, 4, n).transpose(0, 1, 3, 2))
    if fmt == "e4m3":
        words = by_word.astype(ml_dtypes.float8_e4m3fn).view(np.uint8)
    else:
        c = by_word.astype(ml_dtypes.float4_e2m1fn).view(np.uint8) & 0xF
        words = c[..., 0::2] | (c[..., 1::2] << 4)
    return np.ascontiguousarray(words), np.ascontiguousarray(byte.astype(np.uint8).reshape(k // 512, 16, n))


def unpack_weight(words, scales, fmt):
    g, p, n, _ = words.shape
    if fmt == "e4m3":
        vals = np.ascontiguousarray(words).view(ml_dtypes.float8_e4m3fn).astype(np.float64)
    else:
        nib = np.empty((g, p, n, 4), np.uint8)
        nib[..., 0::2] = words & 0xF
        nib[..., 1::2] = words >> 4
        vals = E2M1[nib]
    vals = vals * np.repeat(np.exp2(scales.astype(np.float64) - 127.0), 8, axis=1)[..., None]
    return vals.transpose(0, 1, 3, 2).reshape(g * 512, n)


B, S, D, H, DN, DR, DV, RQ, RKV = 2, 64, 1024, 16, 64, 128, 128, 1536, 8192
THETA = 10000.0
EPS = 1e-6


def rmsnorm(v, w):
    return v * (1.0 / np.sqrt(np.mean(v * v, axis=-1, keepdims=True) + EPS)) * w


def rotate_half(v):
    v1 = v[..., ::2]
    v2 = v[..., 1::2]
    return np.stack((-v2, v1), axis=-1).reshape(v.shape)


def rope_cache():
    inv_freq = 1.0 / THETA ** (np.arange(0, DR, 2) / DR)
    freqs = np.outer(np.arange(S), inv_freq)
    emb = np.concatenate((freqs, freqs), -1)
    return np.cos(emb), np.sin(emb)


def apply_rope(v, cos, sin):
    return v * cos[None, None] + rotate_half(v) * sin[None, None]


def setup_inputs():
    s, t = mx_kscale(D), mx_kscale(RKV)
    x = bf(np.random.standard_normal((B, S, D)) * s)
    Wkva_words, Wkva_scales = pack_weight(np.random.standard_normal((D, RKV + DR)) / np.sqrt(D) / s[:, None], "e4m3")
    kv_a_norm_w = bf((1.0 + 0.1 * np.random.standard_normal(RKV)) * t)
    Wkvb_words, Wkvb_scales = pack_weight(np.random.standard_normal((RKV, H * (DN + DV))) / np.sqrt(RKV) / t[:, None], "e4m3")
    return {"x": x,
            "Wkva_words": Wkva_words,
            "Wkva_scales": Wkva_scales,
            "kv_a_norm_w": kv_a_norm_w,
            "Wkvb_words": Wkvb_words,
            "Wkvb_scales": Wkvb_scales}


def reference(x, Wkva_words, Wkva_scales, kv_a_norm_w, Wkvb_words, Wkvb_scales):
    kv_a = mxq(f64(x), 2, "e4m3") @ unpack_weight(Wkva_words, Wkva_scales, "e4m3")
    kv_latent, k_rope_shared = kv_a[..., :RKV], kv_a[..., RKV:]
    h = rmsnorm(kv_latent, f64(kv_a_norm_w))
    kv = mxq(h, 2, "e4m3") @ unpack_weight(Wkvb_words, Wkvb_scales, "e4m3")
    kv = kv.reshape(B, S, H, DN + DV).transpose(0, 2, 1, 3)
    k_nope, v = kv[..., :DN], kv[..., DN:]
    cos, sin = rope_cache()
    k_rope = apply_rope(k_rope_shared[:, None], cos, sin)
    k_rope = np.broadcast_to(k_rope, (B, H, S, DR))
    k_final = np.concatenate([k_nope, k_rope], -1)
    return k_final, v

@@ -1,0 +1,243 @@
+import math
+
+import concourse.mybir as mybir
+from concourse.masks import make_identity
+
+F32 = mybir.dt.float32
+BF16 = mybir.dt.bfloat16
+I32 = mybir.dt.int32
+U32 = mybir.dt.uint32
+U8 = mybir.dt.uint8
+FP8X4 = mybir.dt.float8_e4m3fn_x4
+ALU = mybir.AluOpType
+ACT = mybir.ActivationFunctionType
+
+B, S, D, H, DN, DR, DV, RKV = 2, 64, 1024, 16, 64, 128, 128, 8192
+THETA = 10000.0
+EPS = 1e-6
+
+P = 128
+PACK = 4
+K_PASS = P * PACK
+BANK = 512
+X_PASSES = D // K_PASS
+H_PASSES = RKV // K_PASS
+A_COLS = RKV + DR
+KV_COLS = H * (DN + DV)
+HALF_COLS = KV_COLS // 2
+HALF_HEADS = H // 2
+HALF_BANKS = HALF_COLS // BANK
+PIECE_PASSES = 2
+PIECE_COLS = HALF_COLS
+PLANES = 4
+QUADRANTS = 4
+RUN = 4
+WEIGHT_BUFS = 11
+
+FLOPS = 2 * P * D * A_COLS + 2 * P * RKV * KV_COLS
+
+
+def tile_multiheadlatentattention_pb_k_kernel(
+    tc, x, Wkva_words, Wkva_scales, kv_a_norm_w, Wkvb_words, Wkvb_scales, out_0, out_1
+):
+    nc = tc.nc
+    wa_words = Wkva_words.rearrange("g p n t -> p g (n t)").bitcast(I32)
+    wb_words = Wkvb_words.rearrange("g p n t -> p g (n t)").bitcast(I32)
+
+    with tc.tile_pool(name="keep", bufs=1) as keep, tc.tile_pool(name="weights", bufs=WEIGHT_BUFS) as weights, tc.tile_pool(
+        name="work", bufs=2
+    ) as work, tc.psum_pool(name="psum", bufs=8) as psum:
+        wa_planes = keep.tile([P, A_COLS], U8, align_bytes=64)
+        wb_planes = keep.tile([P, H_PASSES // PLANES, KV_COLS], U8, align_bytes=64)
+        gain_rows = keep.tile([P, K_PASS], BF16)
+        nc.vector.memset(wa_planes[:].bitcast(I32), 0)
+        nc.vector.memset(gain_rows[:].bitcast(I32), 0)
+        nc.vector.memset(wb_planes[:].rearrange("p a n -> p (a n)").bitcast(I32), 0)
+
+        x_sb = keep.tile([P, D], BF16)
+        for b in range(B):
+            nc.sync.dma_start(out=x_sb[b:P:B, :], in_=x[b])
+        nc.sync.dma_start(out=gain_rows[0:H_PASSES, :], in_=kv_a_norm_w.rearrange("(g k) -> g k", k=K_PASS))
+
+        ident = keep.tile([P, P], F32)
+        make_identity(nc, ident[:])
+        partition_i = keep.tile([P, 1], I32)
+        nc.gpsimd.iota(partition_i[:], pattern=[[0, 1]], base=0, channel_multiplier=1)
+
+        for quad in range(QUADRANTS):
+            nc.gpsimd.dma_start(
+                out=wa_planes[32 * quad : 32 * quad + 4 * X_PASSES, :].bitcast(F32),
+                in_=Wkva_scales[:, 4 * quad : 4 * quad + 4, :].bitcast(F32),
+            )
+        for slot in range(H_PASSES // PLANES):
+            for quad in range(QUADRANTS):
+                nc.gpsimd.dma_start(
+                    out=wb_planes[32 * quad : 32 * quad + 4 * PLANES, slot, :].bitcast(F32),
+                    in_=Wkvb_scales[PLANES * slot : PLANES * (slot + 1), 4 * quad : 4 * quad + 4, :].bitcast(F32),
+                )
+
+        x_words = x_sb[:].bitcast(F32)
+        xt = psum.tile([P, X_PASSES, 2, P], F32, tag="bank")
+        for g in range(X_PASSES):
+            for u in range(2):
+                nc.tensor.transpose(xt[:, g, u, :], x_words[:, (K_PASS // 2) * g + u : (K_PASS // 2) * (g + 1) : 2], ident[:])
+        x_grouped = keep.tile([P, X_PASSES, P, PACK], BF16, align_bytes=64)
+        nc.vector.tensor_copy(out=x_grouped[:].bitcast(F32), in_=xt[:].rearrange("p g u m -> p g m u"))
+        x_codes = keep.tile([P, X_PASSES, P], U32, align_bytes=64)
+        x_planes = keep.tile([P, X_PASSES, P], U8, align_bytes=64)
+        nc.vector.quantize_mx(
+            out=x_codes[:].rearrange("p g m -> p (g m)").bitcast(FP8X4),
+            scales=x_planes[:].rearrange("p g m -> p (g m)"),
+            in_=x_grouped[:].rearrange("p g m t -> p (g m t)"),
+        )
+
+        gain_words = gain_rows[:].bitcast(F32)
+        gt = psum.tile([P, 2, P], F32, tag="bank")
+        for u in range(2):
+            nc.tensor.transpose(gt[:, u, :], gain_words[:, u : K_PASS // 2 : 2], ident[:])
+        gain_kt = keep.tile([P, H_PASSES, PACK], BF16)
+        nc.vector.tensor_copy(out=gain_kt[:].bitcast(F32), in_=gt[:, :, 0:H_PASSES].rearrange("p u g -> p g u"))
+
+        freq = keep.tile([P, DR], F32)
+        nc.vector.memset(freq[:, 0:1], 1.0)
+        for i in range(6):
+            step = 2**i
+            nc.vector.tensor_single_scalar(
+                out=freq[:, step : 2 * step], in_=freq[:, 0:step], scalar=THETA ** (-step / 64.0), op=ALU.mult
+            )
+        nc.vector.tensor_copy(out=freq[:, 64:128], in_=freq[:, 0:64])
+        position_i = keep.tile([P, 1], I32)
+        nc.vector.tensor_single_scalar(out=position_i[:], in_=partition_i[:], scalar=1, op=ALU.arith_shift_right)
+        position_turns = keep.tile([P, 1], F32)
+        nc.vector.tensor_single_scalar(out=position_turns[:], in_=position_i[:], scalar=1.0 / (2.0 * math.pi), op=ALU.mult)
+        turns = keep.tile([P, 2, DR], F32)
+        for c in range(2):
+            nc.vector.tensor_scalar(
+                out=turns[:, c, :], in0=freq[:], scalar1=position_turns[:, 0:1], scalar2=0.25 * c, op0=ALU.mult, op1=ALU.add
+            )
+        turns_flat = turns[:].rearrange("p c j -> p (c j)")
+        whole_i = keep.tile([P, 2 * DR], I32)
+        nc.vector.tensor_copy(out=whole_i[:], in_=turns_flat)
+        whole = keep.tile([P, 2 * DR], F32)
+        nc.vector.tensor_copy(out=whole[:], in_=whole_i[:])
+        frac = keep.tile([P, 2 * DR], F32)
+        nc.vector.tensor_tensor(out=frac[:], in0=turns_flat, in1=whole[:], op=ALU.subtract)
+        minus_frac = keep.tile([P, 2 * DR], F32)
+        nc.vector.scalar_tensor_tensor(
+            out=minus_frac[:], in0=frac[:], scalar=0.5, in1=frac[:], op0=ALU.is_gt, op1=ALU.subtract
+        )
+        sin_cos = keep.tile([P, 2, DR // 2, 2], F32)
+        nc.scalar.activation(
+            out=sin_cos[:].rearrange("p c i e -> p (c i e)"), in_=minus_frac[:], func=ACT.Sin, scale=-2.0 * math.pi
+        )
+
+        c_sorted = keep.tile([P, H_PASSES, PACK, P], F32)
+        sum_squares = keep.tile([P, H_PASSES], F32)
+        rope = keep.tile([P, DR // 2, 2], F32)
+        for first_col in range(0, A_COLS, PIECE_COLS):
+            width = min(PIECE_COLS, A_COLS - first_col)
+            wa = weights.tile([P, PIECE_PASSES, PIECE_COLS], I32, tag="w", align_bytes=64)
+            nc.sync.dma_start(out=wa[:, :, 0:width], in_=wa_words[:, :, first_col : first_col + width])
+            for local in range(0, width, BANK):
+                col = first_col + local
+                n = min(BANK, width - local)
+                acc = psum.tile([P, BANK], F32, tag="bank")
+                for g in range(X_PASSES):
+                    nc.tensor.matmul_mx(
+                        out=acc[:, 0:n],
+                        lhsT=x_codes[:, g, :].bitcast(FP8X4),
+                        lhsT_scale=x_planes[:, g, :],
+                        rhs=wa[:, g, local : local + n].bitcast(FP8X4),
+                        rhs_scale=wa_planes[4 * g : P, col : col + n],
+                        start=(g == 0),
+                        stop=(g == X_PASSES - 1),
+                    )
+                if col < RKV:
+                    bank = col // BANK
+                    nc.vector.tensor_copy(out=c_sorted[:, bank, :, :], in_=acc[:].rearrange("m (p t) -> m t p", t=PACK))
+                    squares = work.tile([P, PACK, P], BF16)
+                    nc.scalar.activation(
+                        out=squares[:], in_=c_sorted[:, bank, :, :], func=ACT.Square, accum_out=sum_squares[:, bank : bank + 1]
+                    )
+                else:
+                    r = acc[:, 0:DR].rearrange("m (i e) -> m i e", e=2)
+                    r_cos = keep.tile([P, DR // 2, 2], F32)
+                    r_sin = keep.tile([P, DR // 2, 2], F32)
+                    nc.vector.tensor_tensor(out=r_cos[:], in0=r, in1=sin_cos[:, 1, :, :], op=ALU.mult)
+                    for e in range(2):
+                        nc.vector.tensor_tensor(
+                            out=r_sin[:, :, e : e + 1], in0=r[:, :, 1 - e : 2 - e], in1=sin_cos[:, 0, :, e : e + 1], op=ALU.mult
+                        )
+                    nc.vector.tensor_tensor(out=rope[:, :, 0:1], in0=r_cos[:, :, 0:1], in1=r_sin[:, :, 0:1], op=ALU.subtract)
+                    nc.vector.tensor_tensor(out=rope[:, :, 1:2], in0=r_cos[:, :, 1:2], in1=r_sin[:, :, 1:2], op=ALU.add)
+                    for b in range(B):
+                        nc.scalar.dma_start(
+                            out=out_0[b, :, :, DN : DN + DR].rearrange("h s f -> s h f"),
+                            in_=rope[b:P:B, :, :].rearrange("m i e -> m (i e)").unsqueeze(1).to_broadcast([S, H, DR]),
+                        )
+
+        mean_square = keep.tile([P, 1], F32)
+        nc.vector.reduce_sum(out=mean_square[:], in_=sum_squares[:], axis=mybir.AxisListType.X)
+        nc.vector.tensor_scalar(
+            out=mean_square[:], in0=mean_square[:], scalar1=1.0 / RKV, scalar2=EPS, op0=ALU.mult, op1=ALU.add
+        )
+        rms = keep.tile([P, 1], F32)
+        nc.scalar.sqrt(out=rms[:], in_=mean_square[:])
+        inv_rms = keep.tile([P, 1], F32)
+        nc.vector.reciprocal(out=inv_rms[:], in_=rms[:])
+
+        h_codes = keep.tile([P, H_PASSES, P], U32, align_bytes=64)
+        h_planes = keep.tile([P, H_PASSES, P], U8, align_bytes=64)
+        for first_pass in range(0, H_PASSES, RUN):
+            h_grouped = work.tile([P, RUN, P, PACK], BF16, align_bytes=64)
+            for i in range(RUN):
+                g = first_pass + i
+                nc.scalar.activation(out=c_sorted[:, g, :, :], in_=c_sorted[:, g, :, :], func=ACT.Copy, scale=inv_rms[:, 0:1])
+                ct = psum.tile([P, PACK, P], F32, tag="bank")
+                for t in range(PACK):
+                    nc.tensor.transpose(ct[:, t, :], c_sorted[:, g, t, :], ident[:])
+                nc.vector.tensor_tensor(
+                    out=h_grouped[:, i, :, :],
+                    in0=ct[:].rearrange("p t m -> p m t"),
+                    in1=gain_kt[:, g, :].unsqueeze(1).to_broadcast([P, P, PACK]),
+                    op=ALU.mult,
+                )
+            passes = slice(first_pass, first_pass + RUN)
+            nc.vector.quantize_mx(
+                out=h_codes[:, passes, :].rearrange("p g m -> p (g m)").bitcast(FP8X4),
+                scales=h_planes[:, passes, :].rearrange("p g m -> p (g m)"),
+                in_=h_grouped[:].rearrange("p g m t -> p (g m t)"),
+            )
+
+        for half in range(2):
+            first_col = half * HALF_COLS
+            kv_acc = [psum.tile([P, BANK], F32, tag="bank", name="kv_acc%d" % j) for j in range(HALF_BANKS)]
+            for first_pass in range(0, H_PASSES, PIECE_PASSES):
+                wb = weights.tile([P, PIECE_PASSES, PIECE_COLS], I32, tag="w", align_bytes=64)
+                nc.sync.dma_start(
+                    out=wb[:], in_=wb_words[:, first_pass : first_pass + PIECE_PASSES, first_col : first_col + PIECE_COLS]
+                )
+                for i in range(PIECE_PASSES):
+                    g = first_pass + i
+                    for j in range(HALF_BANKS):
+                        col = first_col + j * BANK
+                        nc.tensor.matmul_mx(
+                            out=kv_acc[j][:],
+                            lhsT=h_codes[:, g, :].bitcast(FP8X4),
+                            lhsT_scale=h_planes[:, g, :],
+                            rhs=wb[:, i, j * BANK : (j + 1) * BANK].bitcast(FP8X4),
+                            rhs_scale=wb_planes[4 * (g % PLANES) : P, g // PLANES, col : col + BANK],
+                            start=(g == 0),
+                            stop=(g == H_PASSES - 1),
+                        )
+            kv_sb = work.tile([P, HALF_HEADS, DN + DV], F32)
+            kv_flat = kv_sb[:].rearrange("m h f -> m (h f)")
+            for j in range(HALF_BANKS):
+                if j % 2 == 0:
+                    nc.vector.tensor_copy(out=kv_flat[:, j * BANK : (j + 1) * BANK], in_=kv_acc[j][:])
+                else:
+                    nc.scalar.copy(out=kv_flat[:, j * BANK : (j + 1) * BANK], in_=kv_acc[j][:])
+            heads = slice(half * HALF_HEADS, (half + 1) * HALF_HEADS)
+            for b in range(B):
+                nc.scalar.dma_start(out=out_0[b, heads, :, 0:DN].rearrange("h s f -> s h f"), in_=kv_sb[b:P:B, :, 0:DN])
+                nc.scalar.dma_start(out=out_1[b, heads, :, :].rearrange("h s f -> s h f"), in_=kv_sb[b:P:B, :, DN : DN + DV])

@@ -65,16 +65,10 @@ def tile_multiheadlatentattention_pb_k_kernel(
         nc.gpsimd.iota(partition_i[:], pattern=[[0, 1]], base=0, channel_multiplier=1)
 
         for quad in range(QUADRANTS):
-            nc.gpsimd.dma_start(
-                out=wa_planes[32 * quad : 32 * quad + 4 * X_PASSES, :].bitcast(F32),
-                in_=Wkva_scales[:, 4 * quad : 4 * quad + 4, :].bitcast(F32),
+            nc.sync.dma_start(
+                out=wa_planes[32 * quad : 32 * quad + 4 * X_PASSES, :].bitcast(I32),
+                in_=Wkva_scales[:, 4 * quad : 4 * quad + 4, :].bitcast(I32),
             )
-        for slot in range(H_PASSES // PLANES):
-            for quad in range(QUADRANTS):
-                nc.gpsimd.dma_start(
-                    out=wb_planes[32 * quad : 32 * quad + 4 * PLANES, slot, :].bitcast(F32),
-                    in_=Wkvb_scales[PLANES * slot : PLANES * (slot + 1), 4 * quad : 4 * quad + 4, :].bitcast(F32),
-                )
 
         x_words = x_sb[:].bitcast(F32)
         xt = psum.tile([P, X_PASSES, 2, P], F32, tag="bank")
@@ -175,6 +169,13 @@ def tile_multiheadlatentattention_pb_k_kernel(
                             out=out_0[b, :, :, DN : DN + DR].rearrange("h s f -> s h f"),
                             in_=rope[b:P:B, :, :].rearrange("m i e -> m (i e)").unsqueeze(1).to_broadcast([S, H, DR]),
                         )
+
+        for slot in range(H_PASSES // PLANES):
+            for quad in range(QUADRANTS):
+                nc.sync.dma_start(
+                    out=wb_planes[32 * quad : 32 * quad + 4 * PLANES, slot, :].bitcast(I32),
+                    in_=Wkvb_scales[PLANES * slot : PLANES * (slot + 1), 4 * quad : 4 * quad + 4, :].bitcast(I32),
+                )
 
         mean_square = keep.tile([P, 1], F32)
         nc.vector.reduce_sum(out=mean_square[:], in_=sum_squares[:], axis=mybir.AxisListType.X)

@@ -46,12 +46,12 @@ def tile_multiheadlatentattention_pb_k_kernel(
 
     with tc.tile_pool(name="keep", bufs=1) as keep, tc.tile_pool(name="weights", bufs=WEIGHT_BUFS) as weights, tc.tile_pool(
         name="work", bufs=2
-    ) as work, tc.psum_pool(name="psum", bufs=8) as psum:
+    ) as work, tc.psum_pool(name="psum", bufs=8) as psum, tc.manual_schedule():
         wa_planes = keep.tile([P, A_COLS], U8, align_bytes=64)
         wb_planes = keep.tile([P, H_PASSES // PLANES, KV_COLS], U8, align_bytes=64)
         gain_rows = keep.tile([P, K_PASS], BF16)
-        nc.vector.memset(wa_planes[:].bitcast(I32), 0)
         nc.vector.memset(gain_rows[:].bitcast(I32), 0)
+        nc.vector.memset(wa_planes[:].bitcast(I32), 0)
         nc.vector.memset(wb_planes[:].rearrange("p a n -> p (a n)").bitcast(I32), 0)
 
         x_sb = keep.tile([P, D], BF16)
@@ -59,38 +59,37 @@ def tile_multiheadlatentattention_pb_k_kernel(
             nc.sync.dma_start(out=x_sb[b:P:B, :], in_=x[b])
         nc.sync.dma_start(out=gain_rows[0:H_PASSES, :], in_=kv_a_norm_w.rearrange("(g k) -> g k", k=K_PASS))
 
+        wa_tiles = []
+        for first_col in range(0, A_COLS, PIECE_COLS):
+            width = min(PIECE_COLS, A_COLS - first_col)
+            wa = weights.tile([P, PIECE_PASSES, PIECE_COLS], I32, tag="w", align_bytes=64)
+            nc.sync.dma_start(out=wa[:, :, 0:width], in_=wa_words[:, :, first_col : first_col + width])
+            wa_tiles.append(wa)
+        wb_tiles = []
+        for first_col in range(0, KV_COLS, PIECE_COLS):
+            for first_pass in range(0, H_PASSES, PIECE_PASSES):
+                wb = weights.tile([P, PIECE_PASSES, PIECE_COLS], I32, tag="w", align_bytes=64)
+                nc.sync.dma_start(
+                    out=wb[:], in_=wb_words[:, first_pass : first_pass + PIECE_PASSES, first_col : first_col + PIECE_COLS]
+                )
+                wb_tiles.append(wb)
+
         ident = keep.tile([P, P], F32)
         make_identity(nc, ident[:])
         partition_i = keep.tile([P, 1], I32)
         nc.gpsimd.iota(partition_i[:], pattern=[[0, 1]], base=0, channel_multiplier=1)
 
         for quad in range(QUADRANTS):
-            nc.sync.dma_start(
-                out=wa_planes[32 * quad : 32 * quad + 4 * X_PASSES, :].bitcast(I32),
-                in_=Wkva_scales[:, 4 * quad : 4 * quad + 4, :].bitcast(I32),
+            nc.gpsimd.dma_start(
+                out=wa_planes[32 * quad : 32 * quad + 4 * X_PASSES, :].bitcast(F32),
+                in_=Wkva_scales[:, 4 * quad : 4 * quad + 4, :].bitcast(F32),
             )
-
-        x_words = x_sb[:].bitcast(F32)
-        xt = psum.tile([P, X_PASSES, 2, P], F32, tag="bank")
-        for g in range(X_PASSES):
-            for u in range(2):
-                nc.tensor.transpose(xt[:, g, u, :], x_words[:, (K_PASS // 2) * g + u : (K_PASS // 2) * (g + 1) : 2], ident[:])
-        x_grouped = keep.tile([P, X_PASSES, P, PACK], BF16, align_bytes=64)
-        nc.vector.tensor_copy(out=x_grouped[:].bitcast(F32), in_=xt[:].rearrange("p g u m -> p g m u"))
-        x_codes = keep.tile([P, X_PASSES, P], U32, align_bytes=64)
-        x_planes = keep.tile([P, X_PASSES, P], U8, align_bytes=64)
-        nc.vector.quantize_mx(
-            out=x_codes[:].rearrange("p g m -> p (g m)").bitcast(FP8X4),
-            scales=x_planes[:].rearrange("p g m -> p (g m)"),
-            in_=x_grouped[:].rearrange("p g m t -> p (g m t)"),
-        )
-
-        gain_words = gain_rows[:].bitcast(F32)
-        gt = psum.tile([P, 2, P], F32, tag="bank")
-        for u in range(2):
-            nc.tensor.transpose(gt[:, u, :], gain_words[:, u : K_PASS // 2 : 2], ident[:])
-        gain_kt = keep.tile([P, H_PASSES, PACK], BF16)
-        nc.vector.tensor_copy(out=gain_kt[:].bitcast(F32), in_=gt[:, :, 0:H_PASSES].rearrange("p u g -> p g u"))
+        for slot in range(H_PASSES // PLANES):
+            for quad in range(QUADRANTS):
+                nc.gpsimd.dma_start(
+                    out=wb_planes[32 * quad : 32 * quad + 4 * PLANES, slot, :].bitcast(F32),
+                    in_=Wkvb_scales[PLANES * slot : PLANES * (slot + 1), 4 * quad : 4 * quad + 4, :].bitcast(F32),
+                )
 
         freq = keep.tile([P, DR], F32)
         nc.vector.memset(freq[:, 0:1], 1.0)
@@ -125,13 +124,35 @@ def tile_multiheadlatentattention_pb_k_kernel(
             out=sin_cos[:].rearrange("p c i e -> p (c i e)"), in_=minus_frac[:], func=ACT.Sin, scale=-2.0 * math.pi
         )
 
+
+        x_words = x_sb[:].bitcast(F32)
+        xt = psum.tile([P, X_PASSES, 2, P], F32, tag="bank")
+        for g in range(X_PASSES):
+            for u in range(2):
+                nc.tensor.transpose(xt[:, g, u, :], x_words[:, (K_PASS // 2) * g + u : (K_PASS // 2) * (g + 1) : 2], ident[:])
+        x_grouped = keep.tile([P, X_PASSES, P, PACK], BF16, align_bytes=64)
+        nc.vector.tensor_copy(out=x_grouped[:].bitcast(F32), in_=xt[:].rearrange("p g u m -> p g m u"))
+        x_codes = keep.tile([P, X_PASSES, P], U32, align_bytes=64)
+        x_planes = keep.tile([P, X_PASSES, P], U8, align_bytes=64)
+        nc.vector.quantize_mx(
+            out=x_codes[:].rearrange("p g m -> p (g m)").bitcast(FP8X4),
+            scales=x_planes[:].rearrange("p g m -> p (g m)"),
+            in_=x_grouped[:].rearrange("p g m t -> p (g m t)"),
+        )
+
+        gain_words = gain_rows[:].bitcast(F32)
+        gt = psum.tile([P, 2, P], F32, tag="bank")
+        for u in range(2):
+            nc.tensor.transpose(gt[:, u, :], gain_words[:, u : K_PASS // 2 : 2], ident[:])
+        gain_kt = keep.tile([P, H_PASSES, PACK], BF16)
+        nc.vector.tensor_copy(out=gain_kt[:].bitcast(F32), in_=gt[:, :, 0:H_PASSES].rearrange("p u g -> p g u"))
+
         c_sorted = keep.tile([P, H_PASSES, PACK, P], F32)
         sum_squares = keep.tile([P, H_PASSES], F32)
         rope = keep.tile([P, DR // 2, 2], F32)
         for first_col in range(0, A_COLS, PIECE_COLS):
             width = min(PIECE_COLS, A_COLS - first_col)
-            wa = weights.tile([P, PIECE_PASSES, PIECE_COLS], I32, tag="w", align_bytes=64)
-            nc.sync.dma_start(out=wa[:, :, 0:width], in_=wa_words[:, :, first_col : first_col + width])
+            wa = wa_tiles[first_col // PIECE_COLS]
             for local in range(0, width, BANK):
                 col = first_col + local
                 n = min(BANK, width - local)
@@ -165,17 +186,10 @@ def tile_multiheadlatentattention_pb_k_kernel(
                     nc.vector.tensor_tensor(out=rope[:, :, 0:1], in0=r_cos[:, :, 0:1], in1=r_sin[:, :, 0:1], op=ALU.subtract)
                     nc.vector.tensor_tensor(out=rope[:, :, 1:2], in0=r_cos[:, :, 1:2], in1=r_sin[:, :, 1:2], op=ALU.add)
                     for b in range(B):
-                        nc.scalar.dma_start(
+                        nc.sync.dma_start(
                             out=out_0[b, :, :, DN : DN + DR].rearrange("h s f -> s h f"),
                             in_=rope[b:P:B, :, :].rearrange("m i e -> m (i e)").unsqueeze(1).to_broadcast([S, H, DR]),
                         )
-
-        for slot in range(H_PASSES // PLANES):
-            for quad in range(QUADRANTS):
-                nc.sync.dma_start(
-                    out=wb_planes[32 * quad : 32 * quad + 4 * PLANES, slot, :].bitcast(I32),
-                    in_=Wkvb_scales[PLANES * slot : PLANES * (slot + 1), 4 * quad : 4 * quad + 4, :].bitcast(I32),
-                )
 
         mean_square = keep.tile([P, 1], F32)
         nc.vector.reduce_sum(out=mean_square[:], in_=sum_squares[:], axis=mybir.AxisListType.X)
@@ -214,10 +228,7 @@ def tile_multiheadlatentattention_pb_k_kernel(
             first_col = half * HALF_COLS
             kv_acc = [psum.tile([P, BANK], F32, tag="bank", name="kv_acc%d" % j) for j in range(HALF_BANKS)]
             for first_pass in range(0, H_PASSES, PIECE_PASSES):
-                wb = weights.tile([P, PIECE_PASSES, PIECE_COLS], I32, tag="w", align_bytes=64)
-                nc.sync.dma_start(
-                    out=wb[:], in_=wb_words[:, first_pass : first_pass + PIECE_PASSES, first_col : first_col + PIECE_COLS]
-                )
+                wb = wb_tiles[(half * H_PASSES + first_pass) // PIECE_PASSES]
                 for i in range(PIECE_PASSES):
                     g = first_pass + i
                     for j in range(HALF_BANKS):
@@ -240,5 +251,5 @@ def tile_multiheadlatentattention_pb_k_kernel(
                     nc.scalar.copy(out=kv_flat[:, j * BANK : (j + 1) * BANK], in_=kv_acc[j][:])
             heads = slice(half * HALF_HEADS, (half + 1) * HALF_HEADS)
             for b in range(B):
-                nc.scalar.dma_start(out=out_0[b, heads, :, 0:DN].rearrange("h s f -> s h f"), in_=kv_sb[b:P:B, :, 0:DN])
-                nc.scalar.dma_start(out=out_1[b, heads, :, :].rearrange("h s f -> s h f"), in_=kv_sb[b:P:B, :, DN : DN + DV])
+                nc.sync.dma_start(out=out_0[b, heads, :, 0:DN].rearrange("h s f -> s h f"), in_=kv_sb[b:P:B, :, 0:DN])
+                nc.sync.dma_start(out=out_1[b, heads, :, :].rearrange("h s f -> s h f"), in_=kv_sb[b:P:B, :, DN : DN + DV])

@@ -46,7 +46,7 @@ def tile_multiheadlatentattention_pb_k_kernel(
 
     with tc.tile_pool(name="keep", bufs=1) as keep, tc.tile_pool(name="weights", bufs=WEIGHT_BUFS) as weights, tc.tile_pool(
         name="work", bufs=2
-    ) as work, tc.psum_pool(name="psum", bufs=8) as psum, tc.manual_schedule():
+    ) as work, tc.psum_pool(name="psum", bufs=4) as psum, tc.psum_pool(name="kv_psum", bufs=4) as kv_psum, tc.manual_schedule():
         wa_planes = keep.tile([P, A_COLS], U8, align_bytes=64)
         wb_planes = keep.tile([P, H_PASSES // PLANES, KV_COLS], U8, align_bytes=64)
         gain_rows = keep.tile([P, K_PASS], BF16)
@@ -203,7 +203,8 @@ def tile_multiheadlatentattention_pb_k_kernel(
 
         h_codes = keep.tile([P, H_PASSES, P], U32, align_bytes=64)
         h_planes = keep.tile([P, H_PASSES, P], U8, align_bytes=64)
-        for first_pass in range(0, H_PASSES, RUN):
+
+        def quantise_h(first_pass):
             h_grouped = work.tile([P, RUN, P, PACK], BF16, align_bytes=64)
             for i in range(RUN):
                 g = first_pass + i
@@ -224,24 +225,22 @@ def tile_multiheadlatentattention_pb_k_kernel(
                 in_=h_grouped[:].rearrange("p g m t -> p (g m t)"),
             )
 
-        for half in range(2):
-            first_col = half * HALF_COLS
-            kv_acc = [psum.tile([P, BANK], F32, tag="bank", name="kv_acc%d" % j) for j in range(HALF_BANKS)]
-            for first_pass in range(0, H_PASSES, PIECE_PASSES):
-                wb = wb_tiles[(half * H_PASSES + first_pass) // PIECE_PASSES]
-                for i in range(PIECE_PASSES):
-                    g = first_pass + i
-                    for j in range(HALF_BANKS):
-                        col = first_col + j * BANK
-                        nc.tensor.matmul_mx(
-                            out=kv_acc[j][:],
-                            lhsT=h_codes[:, g, :].bitcast(FP8X4),
-                            lhsT_scale=h_planes[:, g, :],
-                            rhs=wb[:, i, j * BANK : (j + 1) * BANK].bitcast(FP8X4),
-                            rhs_scale=wb_planes[4 * (g % PLANES) : P, g // PLANES, col : col + BANK],
-                            start=(g == 0),
-                            stop=(g == H_PASSES - 1),
-                        )
+        def multiply(half, kv_acc, first_pass):
+            for g in range(first_pass, first_pass + RUN):
+                wb = wb_tiles[(half * H_PASSES + g) // PIECE_PASSES]
+                for j in range(HALF_BANKS):
+                    col = half * HALF_COLS + j * BANK
+                    nc.tensor.matmul_mx(
+                        out=kv_acc[j][:],
+                        lhsT=h_codes[:, g, :].bitcast(FP8X4),
+                        lhsT_scale=h_planes[:, g, :],
+                        rhs=wb[:, g % PIECE_PASSES, j * BANK : (j + 1) * BANK].bitcast(FP8X4),
+                        rhs_scale=wb_planes[4 * (g % PLANES) : P, g // PLANES, col : col + BANK],
+                        start=(g == 0),
+                        stop=(g == H_PASSES - 1),
+                    )
+
+        def store(half, kv_acc):
             kv_sb = work.tile([P, HALF_HEADS, DN + DV], F32)
             kv_flat = kv_sb[:].rearrange("m h f -> m (h f)")
             for j in range(HALF_BANKS):
@@ -253,3 +252,15 @@ def tile_multiheadlatentattention_pb_k_kernel(
             for b in range(B):
                 nc.sync.dma_start(out=out_0[b, heads, :, 0:DN].rearrange("h s f -> s h f"), in_=kv_sb[b:P:B, :, 0:DN])
                 nc.sync.dma_start(out=out_1[b, heads, :, :].rearrange("h s f -> s h f"), in_=kv_sb[b:P:B, :, DN : DN + DV])
+
+        kv_first = [kv_psum.tile([P, BANK], F32, tag="kv", name="kv_first%d" % j) for j in range(HALF_BANKS)]
+        quantise_h(0)
+        for first_pass in range(RUN, H_PASSES, RUN):
+            quantise_h(first_pass)
+            multiply(0, kv_first, first_pass - RUN)
+        multiply(0, kv_first, H_PASSES - RUN)
+        store(0, kv_first)
+        kv_last = [kv_psum.tile([P, BANK], F32, tag="kv", name="kv_last%d" % j) for j in range(HALF_BANKS)]
+        for first_pass in range(0, H_PASSES, RUN):
+            multiply(1, kv_last, first_pass)
+        store(1, kv_last)

@@ -27,8 +27,10 @@ KV_COLS = H * (DN + DV)
 HALF_COLS = KV_COLS // 2
 HALF_HEADS = H // 2
 HALF_BANKS = HALF_COLS // BANK
-PIECE_PASSES = 2
-PIECE_COLS = HALF_COLS
+TILE_COLS = KV_COLS
+KV_BANKS = KV_COLS // BANK
+SPLIT_PASSES = 4
+FULL_PASSES = H_PASSES - SPLIT_PASSES
 PLANES = 4
 QUADRANTS = 4
 RUN = 4
@@ -46,7 +48,7 @@ def tile_multiheadlatentattention_pb_k_kernel(
 
     with tc.tile_pool(name="keep", bufs=1) as keep, tc.tile_pool(name="weights", bufs=WEIGHT_BUFS) as weights, tc.tile_pool(
         name="work", bufs=2
-    ) as work, tc.psum_pool(name="psum", bufs=4) as psum, tc.psum_pool(name="kv_psum", bufs=4) as kv_psum, tc.manual_schedule():
+    ) as work, tc.psum_pool(name="psum", bufs=8) as psum, tc.manual_schedule():
         wa_planes = keep.tile([P, A_COLS], U8, align_bytes=64)
         wb_planes = keep.tile([P, H_PASSES // PLANES, KV_COLS], U8, align_bytes=64)
         gain_rows = keep.tile([P, K_PASS], BF16)
@@ -59,20 +61,26 @@ def tile_multiheadlatentattention_pb_k_kernel(
             nc.sync.dma_start(out=x_sb[b:P:B, :], in_=x[b])
         nc.sync.dma_start(out=gain_rows[0:H_PASSES, :], in_=kv_a_norm_w.rearrange("(g k) -> g k", k=K_PASS))
 
-        wa_tiles = []
-        for first_col in range(0, A_COLS, PIECE_COLS):
-            width = min(PIECE_COLS, A_COLS - first_col)
-            wa = weights.tile([P, PIECE_PASSES, PIECE_COLS], I32, tag="w", align_bytes=64)
-            nc.sync.dma_start(out=wa[:, :, 0:width], in_=wa_words[:, :, first_col : first_col + width])
-            wa_tiles.append(wa)
-        wb_tiles = []
-        for first_col in range(0, KV_COLS, PIECE_COLS):
-            for first_pass in range(0, H_PASSES, PIECE_PASSES):
-                wb = weights.tile([P, PIECE_PASSES, PIECE_COLS], I32, tag="w", align_bytes=64)
-                nc.sync.dma_start(
-                    out=wb[:], in_=wb_words[:, first_pass : first_pass + PIECE_PASSES, first_col : first_col + PIECE_COLS]
-                )
-                wb_tiles.append(wb)
+        wa_tiles = {}
+        for first_col in range(0, A_COLS, TILE_COLS):
+            width = min(TILE_COLS, A_COLS - first_col)
+            for g in range(X_PASSES):
+                wa = weights.tile([P, TILE_COLS], I32, tag="w", align_bytes=64)
+                nc.sync.dma_start(out=wa[:, 0:width], in_=wa_words[:, g, first_col : first_col + width])
+                wa_tiles[(first_col, g)] = wa
+        wb_full = []
+        for g in range(FULL_PASSES):
+            wb = weights.tile([P, TILE_COLS], I32, tag="w", align_bytes=64)
+            nc.sync.dma_start(out=wb[:], in_=wb_words[:, g, :])
+            wb_full.append(wb)
+        wb_split = {}
+        for half in range(2):
+            for first_pass in range(FULL_PASSES, H_PASSES, 2):
+                wb = weights.tile([P, TILE_COLS], I32, tag="w", align_bytes=64)
+                for i in range(2):
+                    part = wb[:, i * HALF_COLS : (i + 1) * HALF_COLS]
+                    nc.sync.dma_start(out=part, in_=wb_words[:, first_pass + i, half * HALF_COLS : (half + 1) * HALF_COLS])
+                    wb_split[(half, first_pass + i)] = part
 
         ident = keep.tile([P, P], F32)
         make_identity(nc, ident[:])
@@ -150,23 +158,26 @@ def tile_multiheadlatentattention_pb_k_kernel(
         c_sorted = keep.tile([P, H_PASSES, PACK, P], F32)
         sum_squares = keep.tile([P, H_PASSES], F32)
         rope = keep.tile([P, DR // 2, 2], F32)
-        for first_col in range(0, A_COLS, PIECE_COLS):
-            width = min(PIECE_COLS, A_COLS - first_col)
-            wa = wa_tiles[first_col // PIECE_COLS]
-            for local in range(0, width, BANK):
-                col = first_col + local
-                n = min(BANK, width - local)
-                acc = psum.tile([P, BANK], F32, tag="bank")
-                for g in range(X_PASSES):
+        for first_col in range(0, A_COLS, TILE_COLS):
+            width = min(TILE_COLS, A_COLS - first_col)
+            bank_starts = list(range(0, width, BANK))
+            accs = [psum.tile([P, BANK], F32, tag="bank", name="acc%d" % (local // BANK)) for local in bank_starts]
+            for g in range(X_PASSES):
+                wa = wa_tiles[(first_col, g)]
+                for acc, local in zip(accs, bank_starts):
+                    col = first_col + local
+                    n = min(BANK, width - local)
                     nc.tensor.matmul_mx(
                         out=acc[:, 0:n],
                         lhsT=x_codes[:, g, :].bitcast(FP8X4),
                         lhsT_scale=x_planes[:, g, :],
-                        rhs=wa[:, g, local : local + n].bitcast(FP8X4),
+                        rhs=wa[:, local : local + n].bitcast(FP8X4),
                         rhs_scale=wa_planes[4 * g : P, col : col + n],
                         start=(g == 0),
                         stop=(g == X_PASSES - 1),
                     )
+            for acc, local in zip(accs, bank_starts):
+                col = first_col + local
                 if col < RKV:
                     bank = col // BANK
                     nc.vector.tensor_copy(out=c_sorted[:, bank, :, :], in_=acc[:].rearrange("m (p t) -> m t p", t=PACK))
@@ -203,8 +214,7 @@ def tile_multiheadlatentattention_pb_k_kernel(
 
         h_codes = keep.tile([P, H_PASSES, P], U32, align_bytes=64)
         h_planes = keep.tile([P, H_PASSES, P], U8, align_bytes=64)
-
-        def quantise_h(first_pass):
+        for first_pass in range(0, H_PASSES, RUN):
             h_grouped = work.tile([P, RUN, P, PACK], BF16, align_bytes=64)
             for i in range(RUN):
                 g = first_pass + i
@@ -225,42 +235,34 @@ def tile_multiheadlatentattention_pb_k_kernel(
                 in_=h_grouped[:].rearrange("p g m t -> p (g m t)"),
             )
 
-        def multiply(half, kv_acc, first_pass):
-            for g in range(first_pass, first_pass + RUN):
-                wb = wb_tiles[(half * H_PASSES + g) // PIECE_PASSES]
-                for j in range(HALF_BANKS):
-                    col = half * HALF_COLS + j * BANK
-                    nc.tensor.matmul_mx(
-                        out=kv_acc[j][:],
-                        lhsT=h_codes[:, g, :].bitcast(FP8X4),
-                        lhsT_scale=h_planes[:, g, :],
-                        rhs=wb[:, g % PIECE_PASSES, j * BANK : (j + 1) * BANK].bitcast(FP8X4),
-                        rhs_scale=wb_planes[4 * (g % PLANES) : P, g // PLANES, col : col + BANK],
-                        start=(g == 0),
-                        stop=(g == H_PASSES - 1),
-                    )
+        kv_acc = [psum.tile([P, BANK], F32, tag="bank", name="kv_acc%d" % j) for j in range(KV_BANKS)]
 
-        def store(half, kv_acc):
+        def multiply(g, words, first_bank, banks):
+            for j in range(banks):
+                bank = first_bank + j
+                nc.tensor.matmul_mx(
+                    out=kv_acc[bank][:],
+                    lhsT=h_codes[:, g, :].bitcast(FP8X4),
+                    lhsT_scale=h_planes[:, g, :],
+                    rhs=words[:, j * BANK : (j + 1) * BANK].bitcast(FP8X4),
+                    rhs_scale=wb_planes[4 * (g % PLANES) : P, g // PLANES, bank * BANK : (bank + 1) * BANK],
+                    start=(g == 0),
+                    stop=(g == H_PASSES - 1),
+                )
+
+        for g in range(FULL_PASSES):
+            multiply(g, wb_full[g], 0, KV_BANKS)
+        for half in range(2):
+            for g in range(FULL_PASSES, H_PASSES):
+                multiply(g, wb_split[(half, g)], half * HALF_BANKS, HALF_BANKS)
             kv_sb = work.tile([P, HALF_HEADS, DN + DV], F32)
             kv_flat = kv_sb[:].rearrange("m h f -> m (h f)")
             for j in range(HALF_BANKS):
                 if j % 2 == 0:
-                    nc.vector.tensor_copy(out=kv_flat[:, j * BANK : (j + 1) * BANK], in_=kv_acc[j][:])
+                    nc.vector.tensor_copy(out=kv_flat[:, j * BANK : (j + 1) * BANK], in_=kv_acc[half * HALF_BANKS + j][:])
                 else:
-                    nc.scalar.copy(out=kv_flat[:, j * BANK : (j + 1) * BANK], in_=kv_acc[j][:])
+                    nc.scalar.copy(out=kv_flat[:, j * BANK : (j + 1) * BANK], in_=kv_acc[half * HALF_BANKS + j][:])
             heads = slice(half * HALF_HEADS, (half + 1) * HALF_HEADS)
             for b in range(B):
                 nc.sync.dma_start(out=out_0[b, heads, :, 0:DN].rearrange("h s f -> s h f"), in_=kv_sb[b:P:B, :, 0:DN])
                 nc.sync.dma_start(out=out_1[b, heads, :, :].rearrange("h s f -> s h f"), in_=kv_sb[b:P:B, :, DN : DN + DV])
-
-        kv_first = [kv_psum.tile([P, BANK], F32, tag="kv", name="kv_first%d" % j) for j in range(HALF_BANKS)]
-        quantise_h(0)
-        for first_pass in range(RUN, H_PASSES, RUN):
-            quantise_h(first_pass)
-            multiply(0, kv_first, first_pass - RUN)
-        multiply(0, kv_first, H_PASSES - RUN)
-        store(0, kv_first)
-        kv_last = [kv_psum.tile([P, BANK], F32, tag="kv", name="kv_last%d" % j) for j in range(HALF_BANKS)]
-        for first_pass in range(0, H_PASSES, RUN):
-            multiply(1, kv_last, first_pass)
-        store(1, kv_last)

@@ -33,8 +33,8 @@ SPLIT_PASSES = 4
 FULL_PASSES = H_PASSES - SPLIT_PASSES
 PLANES = 4
 QUADRANTS = 4
-RUN = 4
-WEIGHT_BUFS = 11
+BATCH = 3
+WEIGHT_BUFS = 10
 
 FLOPS = 2 * P * D * A_COLS + 2 * P * RKV * KV_COLS
 
@@ -131,7 +131,8 @@ def tile_multiheadlatentattention_pb_k_kernel(
         nc.scalar.activation(
             out=sin_cos[:].rearrange("p c i e -> p (c i e)"), in_=minus_frac[:], func=ACT.Sin, scale=-2.0 * math.pi
         )
-
+        first_sqrt = keep.tile([P, 1], F32)
+        nc.scalar.sqrt(out=first_sqrt[:], in_=freq[:, 0:1])
 
         x_words = x_sb[:].bitcast(F32)
         xt = psum.tile([P, X_PASSES, 2, P], F32, tag="bank")
@@ -155,85 +156,126 @@ def tile_multiheadlatentattention_pb_k_kernel(
         gain_kt = keep.tile([P, H_PASSES, PACK], BF16)
         nc.vector.tensor_copy(out=gain_kt[:].bitcast(F32), in_=gt[:, :, 0:H_PASSES].rearrange("p u g -> p g u"))
 
-        c_sorted = keep.tile([P, H_PASSES, PACK, P], F32)
+        c_gain = keep.tile([P, H_PASSES, P, PACK], F32)
         sum_squares = keep.tile([P, H_PASSES], F32)
-        rope = keep.tile([P, DR // 2, 2], F32)
-        for first_col in range(0, A_COLS, TILE_COLS):
-            width = min(TILE_COLS, A_COLS - first_col)
-            bank_starts = list(range(0, width, BANK))
-            accs = [psum.tile([P, BANK], F32, tag="bank", name="acc%d" % (local // BANK)) for local in bank_starts]
-            for g in range(X_PASSES):
-                wa = wa_tiles[(first_col, g)]
-                for acc, local in zip(accs, bank_starts):
-                    col = first_col + local
-                    n = min(BANK, width - local)
-                    nc.tensor.matmul_mx(
-                        out=acc[:, 0:n],
-                        lhsT=x_codes[:, g, :].bitcast(FP8X4),
-                        lhsT_scale=x_planes[:, g, :],
-                        rhs=wa[:, local : local + n].bitcast(FP8X4),
-                        rhs_scale=wa_planes[4 * g : P, col : col + n],
-                        start=(g == 0),
-                        stop=(g == X_PASSES - 1),
-                    )
-            for acc, local in zip(accs, bank_starts):
-                col = first_col + local
-                if col < RKV:
-                    bank = col // BANK
-                    nc.vector.tensor_copy(out=c_sorted[:, bank, :, :], in_=acc[:].rearrange("m (p t) -> m t p", t=PACK))
-                    squares = work.tile([P, PACK, P], BF16)
-                    nc.scalar.activation(
-                        out=squares[:], in_=c_sorted[:, bank, :, :], func=ACT.Square, accum_out=sum_squares[:, bank : bank + 1]
-                    )
-                else:
-                    r = acc[:, 0:DR].rearrange("m (i e) -> m i e", e=2)
-                    r_cos = keep.tile([P, DR // 2, 2], F32)
-                    r_sin = keep.tile([P, DR // 2, 2], F32)
-                    nc.vector.tensor_tensor(out=r_cos[:], in0=r, in1=sin_cos[:, 1, :, :], op=ALU.mult)
-                    for e in range(2):
-                        nc.vector.tensor_tensor(
-                            out=r_sin[:, :, e : e + 1], in0=r[:, :, 1 - e : 2 - e], in1=sin_cos[:, 0, :, e : e + 1], op=ALU.mult
-                        )
-                    nc.vector.tensor_tensor(out=rope[:, :, 0:1], in0=r_cos[:, :, 0:1], in1=r_sin[:, :, 0:1], op=ALU.subtract)
-                    nc.vector.tensor_tensor(out=rope[:, :, 1:2], in0=r_cos[:, :, 1:2], in1=r_sin[:, :, 1:2], op=ALU.add)
-                    for b in range(B):
-                        nc.sync.dma_start(
-                            out=out_0[b, :, :, DN : DN + DR].rearrange("h s f -> s h f"),
-                            in_=rope[b:P:B, :, :].rearrange("m i e -> m (i e)").unsqueeze(1).to_broadcast([S, H, DR]),
-                        )
+        c_tiles = {}
 
-        mean_square = keep.tile([P, 1], F32)
-        nc.vector.reduce_sum(out=mean_square[:], in_=sum_squares[:], axis=mybir.AxisListType.X)
+        def multiply_a(bank):
+            col = bank * BANK
+            n = min(BANK, A_COLS - col)
+            first_col = col // TILE_COLS * TILE_COLS
+            acc = psum.tile([P, BANK], F32, tag="bank", name="acc")
+            for g in range(X_PASSES):
+                nc.tensor.matmul_mx(
+                    out=acc[:, 0:n],
+                    lhsT=x_codes[:, g, :].bitcast(FP8X4),
+                    lhsT_scale=x_planes[:, g, :],
+                    rhs=wa_tiles[(first_col, g)][:, col - first_col : col - first_col + n].bitcast(FP8X4),
+                    rhs_scale=wa_planes[4 * g : P, col : col + n],
+                    start=(g == 0),
+                    stop=(g == X_PASSES - 1),
+                )
+            return acc
+
+        def copy_c(bank, acc, copy):
+            c_tiles[bank] = work.tile([P, PACK, P], F32, tag="c", bufs=2 * BATCH, name="c_tile")
+            copy(out=c_tiles[bank][:], in_=acc[:].rearrange("m (p t) -> m t p", t=PACK))
+
+        def add_squares(bank):
+            squares = work.tile([P, PACK, P], BF16)
+            nc.scalar.activation(
+                out=squares[:], in_=c_tiles[bank][:], func=ACT.Square, accum_out=sum_squares[:, bank : bank + 1]
+            )
+
+        def transpose_c(bank):
+            ct = psum.tile([P, PACK, P], F32, tag="bank", name="ct")
+            for t in range(PACK):
+                nc.tensor.transpose(ct[:, t, :], c_tiles[bank][:, t, :], ident[:])
+            return ct
+
+        def apply_gain(bank, ct):
+            nc.vector.tensor_tensor(
+                out=c_gain[:, bank, :, :],
+                in0=ct[:].rearrange("p t m -> p m t"),
+                in1=gain_kt[:, bank, :].unsqueeze(1).to_broadcast([P, P, PACK]),
+                op=ALU.mult,
+            )
+
+        before = []
+        for first_bank in range(0, H_PASSES, BATCH):
+            banks = list(range(first_bank, min(first_bank + BATCH, H_PASSES)))
+            accs = [multiply_a(bank) for bank in banks]
+            if banks[-1] == H_PASSES - 1:
+                r_acc = multiply_a(H_PASSES)
+            cts = [transpose_c(bank) for bank in before]
+            for bank, acc in zip(banks, accs):
+                copy_c(bank, acc, nc.vector.tensor_copy if bank == first_bank else nc.scalar.copy)
+            for bank in banks:
+                add_squares(bank)
+            for bank, ct in zip(before, cts):
+                apply_gain(bank, ct)
+            before = banks
+        for bank in before:
+            apply_gain(bank, transpose_c(bank))
+
+        others = keep.tile([P, 1], F32)
+        nc.vector.reduce_sum(out=others[:], in_=sum_squares[:, 0 : H_PASSES - 1], axis=mybir.AxisListType.X)
+        others_mean = keep.tile([P, 1], F32)
         nc.vector.tensor_scalar(
-            out=mean_square[:], in0=mean_square[:], scalar1=1.0 / RKV, scalar2=EPS, op0=ALU.mult, op1=ALU.add
+            out=others_mean[:], in0=others[:], scalar1=1.0 / RKV, scalar2=EPS, op0=ALU.mult, op1=ALU.add
         )
         rms = keep.tile([P, 1], F32)
-        nc.scalar.sqrt(out=rms[:], in_=mean_square[:])
+        nc.scalar.activation(
+            out=rms[:], in_=sum_squares[:, H_PASSES - 1 : H_PASSES], func=ACT.Sqrt, scale=1.0 / RKV, bias=others_mean[:, 0:1]
+        )
+
+        rope = keep.tile([P, DR // 2, 2], F32)
+        r = r_acc[:, 0:DR].rearrange("m (i e) -> m i e", e=2)
+        r_cos = keep.tile([P, DR // 2, 2], F32)
+        r_sin = keep.tile([P, DR // 2, 2], F32)
+        nc.vector.tensor_tensor(out=r_cos[:], in0=r, in1=sin_cos[:, 1, :, :], op=ALU.mult)
+        for e in range(2):
+            nc.vector.tensor_tensor(
+                out=r_sin[:, :, e : e + 1], in0=r[:, :, 1 - e : 2 - e], in1=sin_cos[:, 0, :, e : e + 1], op=ALU.mult
+            )
+        nc.vector.tensor_tensor(out=rope[:, :, 0:1], in0=r_cos[:, :, 0:1], in1=r_sin[:, :, 0:1], op=ALU.subtract)
+        nc.vector.tensor_tensor(out=rope[:, :, 1:2], in0=r_cos[:, :, 1:2], in1=r_sin[:, :, 1:2], op=ALU.add)
+        for b in range(B):
+            nc.sync.dma_start(
+                out=out_0[b, :, :, DN : DN + DR].rearrange("h s f -> s h f"),
+                in_=rope[b:P:B, :, :].rearrange("m i e -> m (i e)").unsqueeze(1).to_broadcast([S, H, DR]),
+            )
+
         inv_rms = keep.tile([P, 1], F32)
         nc.vector.reciprocal(out=inv_rms[:], in_=rms[:])
+        inv_row = psum.tile([P, P], F32, tag="bank")
+        nc.tensor.transpose(inv_row[:], inv_rms[:, 0:1].to_broadcast([P, P]), ident[:])
 
         h_codes = keep.tile([P, H_PASSES, P], U32, align_bytes=64)
         h_planes = keep.tile([P, H_PASSES, P], U8, align_bytes=64)
-        for first_pass in range(0, H_PASSES, RUN):
-            h_grouped = work.tile([P, RUN, P, PACK], BF16, align_bytes=64)
-            for i in range(RUN):
-                g = first_pass + i
-                nc.scalar.activation(out=c_sorted[:, g, :, :], in_=c_sorted[:, g, :, :], func=ACT.Copy, scale=inv_rms[:, 0:1])
-                ct = psum.tile([P, PACK, P], F32, tag="bank")
-                for t in range(PACK):
-                    nc.tensor.transpose(ct[:, t, :], c_sorted[:, g, t, :], ident[:])
-                nc.vector.tensor_tensor(
-                    out=h_grouped[:, i, :, :],
-                    in0=ct[:].rearrange("p t m -> p m t"),
-                    in1=gain_kt[:, g, :].unsqueeze(1).to_broadcast([P, P, PACK]),
-                    op=ALU.mult,
-                )
-            passes = slice(first_pass, first_pass + RUN)
-            nc.vector.quantize_mx(
-                out=h_codes[:, passes, :].rearrange("p g m -> p (g m)").bitcast(FP8X4),
-                scales=h_planes[:, passes, :].rearrange("p g m -> p (g m)"),
-                in_=h_grouped[:].rearrange("p g m t -> p (g m t)"),
+        h_tiles = {}
+
+        def scale_h(g):
+            h_tiles[g] = work.tile([P, P, PACK], BF16, tag="h", bufs=3, align_bytes=64, name="h_tile")
+            nc.vector.tensor_tensor(
+                out=h_tiles[g][:],
+                in0=c_gain[:, g, :, :],
+                in1=inv_row[:].unsqueeze(2).to_broadcast([P, P, PACK]),
+                op=ALU.mult,
             )
+
+        def quantize_h(g):
+            nc.vector.quantize_mx(
+                out=h_codes[:, g, :].bitcast(FP8X4),
+                scales=h_planes[:, g, :],
+                in_=h_tiles[g][:].rearrange("p m t -> p (m t)"),
+            )
+
+        scale_h(0)
+        for g in range(1, H_PASSES):
+            scale_h(g)
+            quantize_h(g - 1)
+        quantize_h(H_PASSES - 1)
 
         kv_acc = [psum.tile([P, BANK], F32, tag="bank", name="kv_acc%d" % j) for j in range(KV_BANKS)]
 

@@ -24,11 +24,9 @@ X_PASSES = D // K_PASS
 H_PASSES = RKV // K_PASS
 A_COLS = RKV + DR
 KV_COLS = H * (DN + DV)
-HALF_COLS = KV_COLS // 2
-HALF_HEADS = H // 2
-HALF_BANKS = HALF_COLS // BANK
+PART_HEADS = (12, 4)
+PART_FIRST_HEAD = (0, 12)
 TILE_COLS = KV_COLS
-KV_BANKS = KV_COLS // BANK
 SPLIT_PASSES = 4
 FULL_PASSES = H_PASSES - SPLIT_PASSES
 PLANES = 4
@@ -74,13 +72,17 @@ def tile_multiheadlatentattention_pb_k_kernel(
             nc.sync.dma_start(out=wb[:], in_=wb_words[:, g, :])
             wb_full.append(wb)
         wb_split = {}
-        for half in range(2):
-            for first_pass in range(FULL_PASSES, H_PASSES, 2):
-                wb = weights.tile([P, TILE_COLS], I32, tag="w", align_bytes=64)
-                for i in range(2):
-                    part = wb[:, i * HALF_COLS : (i + 1) * HALF_COLS]
-                    nc.sync.dma_start(out=part, in_=wb_words[:, first_pass + i, half * HALF_COLS : (half + 1) * HALF_COLS])
-                    wb_split[(half, first_pass + i)] = part
+        for part in range(2):
+            first_col = PART_FIRST_HEAD[part] * (DN + DV)
+            width = PART_HEADS[part] * (DN + DV)
+            in_tile = TILE_COLS // width
+            for g in range(FULL_PASSES, H_PASSES):
+                slot = (g - FULL_PASSES) % in_tile
+                if slot == 0:
+                    wb = weights.tile([P, TILE_COLS], I32, tag="w", align_bytes=64)
+                words = wb[:, slot * width : (slot + 1) * width]
+                nc.sync.dma_start(out=words, in_=wb_words[:, g, first_col : first_col + width])
+                wb_split[(part, g)] = words
 
         ident = keep.tile([P, P], F32)
         make_identity(nc, ident[:])
@@ -277,34 +279,38 @@ def tile_multiheadlatentattention_pb_k_kernel(
             quantize_h(g - 1)
         quantize_h(H_PASSES - 1)
 
-        kv_acc = [psum.tile([P, BANK], F32, tag="bank", name="kv_acc%d" % j) for j in range(KV_BANKS)]
+        chunks = []
+        for part in range(2):
+            width = PART_HEADS[part] * (DN + DV)
+            chunks.append(
+                [(at, min(BANK, width - at), psum.tile([P, BANK], F32, tag="bank", name="kv_acc")) for at in range(0, width, BANK)]
+            )
 
-        def multiply(g, words, first_bank, banks):
-            for j in range(banks):
-                bank = first_bank + j
+        def multiply(g, part, words, offset):
+            first_col = PART_FIRST_HEAD[part] * (DN + DV)
+            for at, n, acc in chunks[part]:
                 nc.tensor.matmul_mx(
-                    out=kv_acc[bank][:],
+                    out=acc[:, 0:n],
                     lhsT=h_codes[:, g, :].bitcast(FP8X4),
                     lhsT_scale=h_planes[:, g, :],
-                    rhs=words[:, j * BANK : (j + 1) * BANK].bitcast(FP8X4),
-                    rhs_scale=wb_planes[4 * (g % PLANES) : P, g // PLANES, bank * BANK : (bank + 1) * BANK],
+                    rhs=words[:, offset + at : offset + at + n].bitcast(FP8X4),
+                    rhs_scale=wb_planes[4 * (g % PLANES) : P, g // PLANES, first_col + at : first_col + at + n],
                     start=(g == 0),
                     stop=(g == H_PASSES - 1),
                 )
 
         for g in range(FULL_PASSES):
-            multiply(g, wb_full[g], 0, KV_BANKS)
-        for half in range(2):
+            for part in range(2):
+                multiply(g, part, wb_full[g], PART_FIRST_HEAD[part] * (DN + DV))
+        for part in range(2):
             for g in range(FULL_PASSES, H_PASSES):
-                multiply(g, wb_split[(half, g)], half * HALF_BANKS, HALF_BANKS)
-            kv_sb = work.tile([P, HALF_HEADS, DN + DV], F32)
+                multiply(g, part, wb_split[(part, g)], 0)
+            kv_sb = work.tile([P, PART_HEADS[part], DN + DV], F32, tag="kv%d" % part, bufs=1, name="kv_sb")
             kv_flat = kv_sb[:].rearrange("m h f -> m (h f)")
-            for j in range(HALF_BANKS):
-                if j % 2 == 0:
-                    nc.vector.tensor_copy(out=kv_flat[:, j * BANK : (j + 1) * BANK], in_=kv_acc[half * HALF_BANKS + j][:])
-                else:
-                    nc.scalar.copy(out=kv_flat[:, j * BANK : (j + 1) * BANK], in_=kv_acc[half * HALF_BANKS + j][:])
-            heads = slice(half * HALF_HEADS, (half + 1) * HALF_HEADS)
+            for i, (at, n, acc) in enumerate(chunks[part]):
+                copy = nc.vector.tensor_copy if i % 2 == 0 else nc.scalar.copy
+                copy(out=kv_flat[:, at : at + n], in_=acc[:, 0:n])
+            heads = slice(PART_FIRST_HEAD[part], PART_FIRST_HEAD[part] + PART_HEADS[part])
             for b in range(B):
                 nc.sync.dma_start(out=out_0[b, heads, :, 0:DN].rearrange("h s f -> s h f"), in_=kv_sb[b:P:B, :, 0:DN])
                 nc.sync.dma_start(out=out_1[b, heads, :, :].rearrange("h s f -> s h f"), in_=kv_sb[b:P:B, :, DN : DN + DV])

@@ -27,12 +27,13 @@ KV_COLS = H * (DN + DV)
 PART_HEADS = (12, 4)
 PART_FIRST_HEAD = (0, 12)
 TILE_COLS = KV_COLS
+TILE_PASSES = 2
 SPLIT_PASSES = 4
 FULL_PASSES = H_PASSES - SPLIT_PASSES
 PLANES = 4
 QUADRANTS = 4
 BATCH = 3
-WEIGHT_BUFS = 10
+WEIGHT_BUFS = 5
 
 FLOPS = 2 * P * D * A_COLS + 2 * P * RKV * KV_COLS
 
@@ -62,27 +63,27 @@ def tile_multiheadlatentattention_pb_k_kernel(
         wa_tiles = {}
         for first_col in range(0, A_COLS, TILE_COLS):
             width = min(TILE_COLS, A_COLS - first_col)
-            for g in range(X_PASSES):
-                wa = weights.tile([P, TILE_COLS], I32, tag="w", align_bytes=64)
-                nc.sync.dma_start(out=wa[:, 0:width], in_=wa_words[:, g, first_col : first_col + width])
-                wa_tiles[(first_col, g)] = wa
+            wa = weights.tile([P, TILE_PASSES, TILE_COLS], I32, tag="w", align_bytes=64)
+            nc.sync.dma_start(out=wa[:, :, 0:width], in_=wa_words[:, :, first_col : first_col + width])
+            wa_tiles[first_col] = wa
         wb_full = []
-        for g in range(FULL_PASSES):
-            wb = weights.tile([P, TILE_COLS], I32, tag="w", align_bytes=64)
-            nc.sync.dma_start(out=wb[:], in_=wb_words[:, g, :])
-            wb_full.append(wb)
+        for first_pass in range(0, FULL_PASSES, TILE_PASSES):
+            wb = weights.tile([P, TILE_PASSES, TILE_COLS], I32, tag="w", align_bytes=64)
+            nc.sync.dma_start(out=wb[:], in_=wb_words[:, first_pass : first_pass + TILE_PASSES, :])
+            wb_full.extend([wb[:, i, :] for i in range(TILE_PASSES)])
         wb_split = {}
         for part in range(2):
             first_col = PART_FIRST_HEAD[part] * (DN + DV)
             width = PART_HEADS[part] * (DN + DV)
-            in_tile = TILE_COLS // width
-            for g in range(FULL_PASSES, H_PASSES):
-                slot = (g - FULL_PASSES) % in_tile
-                if slot == 0:
-                    wb = weights.tile([P, TILE_COLS], I32, tag="w", align_bytes=64)
-                words = wb[:, slot * width : (slot + 1) * width]
-                nc.sync.dma_start(out=words, in_=wb_words[:, g, first_col : first_col + width])
-                wb_split[(part, g)] = words
+            for first_pass in range(FULL_PASSES, H_PASSES, TILE_PASSES):
+                if part == 0 or first_pass == FULL_PASSES:
+                    wb = weights.tile([P, TILE_PASSES * TILE_COLS], I32, tag="w", align_bytes=64)
+                for i in range(TILE_PASSES):
+                    slot = i if part == 0 else first_pass - FULL_PASSES + i
+                    words = wb[:, slot * width : (slot + 1) * width]
+                    g = first_pass + i
+                    nc.sync.dma_start(out=words, in_=wb_words[:, g, first_col : first_col + width])
+                    wb_split[(part, g)] = words
 
         ident = keep.tile([P, P], F32)
         make_identity(nc, ident[:])
@@ -172,7 +173,7 @@ def tile_multiheadlatentattention_pb_k_kernel(
                     out=acc[:, 0:n],
                     lhsT=x_codes[:, g, :].bitcast(FP8X4),
                     lhsT_scale=x_planes[:, g, :],
-                    rhs=wa_tiles[(first_col, g)][:, col - first_col : col - first_col + n].bitcast(FP8X4),
+                    rhs=wa_tiles[first_col][:, g, col - first_col : col - first_col + n].bitcast(FP8X4),
                     rhs_scale=wa_planes[4 * g : P, col : col + n],
                     start=(g == 0),
                     stop=(g == X_PASSES - 1),

@@ -90,11 +90,13 @@ def tile_multiheadlatentattention_pb_k_kernel(
         partition_i = keep.tile([P, 1], I32)
         nc.gpsimd.iota(partition_i[:], pattern=[[0, 1]], base=0, channel_multiplier=1)
 
-        for quad in range(QUADRANTS):
-            nc.gpsimd.dma_start(
-                out=wa_planes[32 * quad : 32 * quad + 4 * X_PASSES, :].bitcast(F32),
-                in_=Wkva_scales[:, 4 * quad : 4 * quad + 4, :].bitcast(F32),
-            )
+        for col in range(0, A_COLS, A_COLS // 2):
+            cols = slice(col, col + A_COLS // 2)
+            for quad in range(QUADRANTS):
+                nc.gpsimd.dma_start(
+                    out=wa_planes[32 * quad : 32 * quad + 4 * X_PASSES, cols].bitcast(F32),
+                    in_=Wkva_scales[:, 4 * quad : 4 * quad + 4, cols].bitcast(F32),
+                )
         for slot in range(H_PASSES // PLANES):
             for quad in range(QUADRANTS):
                 nc.gpsimd.dma_start(

@@ -28,9 +28,11 @@ PART_HEADS = (12, 4)
 PART_FIRST_HEAD = (0, 12)
 TILE_COLS = KV_COLS
 TILE_PASSES = 2
-SPLIT_PASSES = 4
+SPLIT_PASSES = 8
 FULL_PASSES = H_PASSES - SPLIT_PASSES
 PLANES = 4
+BLOCK = DN
+HEAD_BLOCKS = (DN + DV) // BLOCK
 QUADRANTS = 4
 BATCH = 3
 WEIGHT_BUFS = 5
@@ -126,11 +128,11 @@ def tile_multiheadlatentattention_pb_k_kernel(
         nc.vector.tensor_copy(out=whole_i[:], in_=turns_flat)
         whole = keep.tile([P, 2 * DR], F32)
         nc.vector.tensor_copy(out=whole[:], in_=whole_i[:])
-        frac = keep.tile([P, 2 * DR], F32)
-        nc.vector.tensor_tensor(out=frac[:], in0=turns_flat, in1=whole[:], op=ALU.subtract)
-        minus_frac = keep.tile([P, 2 * DR], F32)
+        frac = turns_flat
+        nc.vector.tensor_tensor(out=frac, in0=turns_flat, in1=whole[:], op=ALU.subtract)
+        minus_frac = whole
         nc.vector.scalar_tensor_tensor(
-            out=minus_frac[:], in0=frac[:], scalar=0.5, in1=frac[:], op0=ALU.is_gt, op1=ALU.subtract
+            out=minus_frac[:], in0=frac, scalar=0.5, in1=frac, op0=ALU.is_gt, op1=ALU.subtract
         )
         sin_cos = keep.tile([P, 2, DR // 2, 2], F32)
         nc.scalar.activation(
@@ -245,11 +247,14 @@ def tile_multiheadlatentattention_pb_k_kernel(
             )
         nc.vector.tensor_tensor(out=rope[:, :, 0:1], in0=r_cos[:, :, 0:1], in1=r_sin[:, :, 0:1], op=ALU.subtract)
         nc.vector.tensor_tensor(out=rope[:, :, 1:2], in0=r_cos[:, :, 1:2], in1=r_sin[:, :, 1:2], op=ALU.add)
-        for b in range(B):
-            nc.sync.dma_start(
-                out=out_0[b, :, :, DN : DN + DR].rearrange("h s f -> s h f"),
-                in_=rope[b:P:B, :, :].rearrange("m i e -> m (i e)").unsqueeze(1).to_broadcast([S, H, DR]),
+        k_tiles = []
+        for heads in PART_HEADS:
+            k_sb = keep.tile([P, heads, DN + DR], F32, name="k_sb%d" % len(k_tiles))
+            nc.vector.tensor_copy(
+                out=k_sb[:, :, DN : DN + DR],
+                in_=rope[:].rearrange("m i e -> m (i e)").unsqueeze(1).to_broadcast([P, heads, DR]),
             )
+            k_tiles.append(k_sb)
 
         inv_rms = keep.tile([P, 1], F32)
         nc.vector.reciprocal(out=inv_rms[:], in_=rms[:])
@@ -308,12 +313,21 @@ def tile_multiheadlatentattention_pb_k_kernel(
         for part in range(2):
             for g in range(FULL_PASSES, H_PASSES):
                 multiply(g, part, wb_split[(part, g)], 0)
-            kv_sb = work.tile([P, PART_HEADS[part], DN + DV], F32, tag="kv%d" % part, bufs=1, name="kv_sb")
-            kv_flat = kv_sb[:].rearrange("m h f -> m (h f)")
+            k_sb = k_tiles[part]
+            v_sb = work.tile([P, PART_HEADS[part], DV], F32, tag="v%d" % part, bufs=1, name="v_sb")
             for i, (at, n, acc) in enumerate(chunks[part]):
                 copy = nc.vector.tensor_copy if i % 2 == 0 else nc.scalar.copy
-                copy(out=kv_flat[:, at : at + n], in_=acc[:, 0:n])
+                blocks = acc[:, 0:n].rearrange("m (j f) -> m j f", f=BLOCK)
+                for kind in range(HEAD_BLOCKS):
+                    first = (kind - at // BLOCK) % HEAD_BLOCKS
+                    found = blocks[:, first : n // BLOCK : HEAD_BLOCKS, :]
+                    head = (at // BLOCK + first) // HEAD_BLOCKS
+                    heads = slice(head, head + found.shape[1])
+                    if kind == 0:
+                        copy(out=k_sb[:, heads, 0:DN], in_=found)
+                    else:
+                        copy(out=v_sb[:, heads, (kind - 1) * BLOCK : kind * BLOCK], in_=found)
             heads = slice(PART_FIRST_HEAD[part], PART_FIRST_HEAD[part] + PART_HEADS[part])
             for b in range(B):
-                nc.sync.dma_start(out=out_0[b, heads, :, 0:DN].rearrange("h s f -> s h f"), in_=kv_sb[b:P:B, :, 0:DN])
-                nc.sync.dma_start(out=out_1[b, heads, :, :].rearrange("h s f -> s h f"), in_=kv_sb[b:P:B, :, DN : DN + DV])
+                nc.sync.dma_start(out=out_0[b, heads, :, :].rearrange("h s f -> s h f"), in_=k_sb[b:P:B, :, :])
+                nc.sync.dma_start(out=out_1[b, heads, :, :].rearrange("h s f -> s h f"), in_=v_sb[b:P:B, :, :])

@@ -34,6 +34,7 @@ PLANES = 4
 BLOCK = DN
 HEAD_BLOCKS = (DN + DV) // BLOCK
 QUADRANTS = 4
+HOLD_WORDS = 16
 BATCH = 3
 WEIGHT_BUFS = 5
 
@@ -62,15 +63,52 @@ def tile_multiheadlatentattention_pb_k_kernel(
             nc.sync.dma_start(out=x_sb[b:P:B, :], in_=x[b])
         nc.sync.dma_start(out=gain_rows[0:H_PASSES, :], in_=kv_a_norm_w.rearrange("(g k) -> g k", k=K_PASS))
 
+        ident = keep.tile([P, P], F32)
+        make_identity(nc, ident[:])
+        partition_i = keep.tile([P, 1], I32)
+        nc.gpsimd.iota(partition_i[:], pattern=[[0, 1]], base=0, channel_multiplier=1)
+
+        def load_wa_planes(cols):
+            for quad in range(QUADRANTS):
+                nc.gpsimd.dma_start(
+                    out=wa_planes[32 * quad : 32 * quad + 4 * X_PASSES, cols].bitcast(F32),
+                    in_=Wkva_scales[:, 4 * quad : 4 * quad + 4, cols].bitcast(F32),
+                )
+
+        def load_wb_planes(slot):
+            for quad in range(QUADRANTS):
+                nc.gpsimd.dma_start(
+                    out=wb_planes[32 * quad : 32 * quad + 4 * PLANES, slot, :].bitcast(F32),
+                    in_=Wkvb_scales[PLANES * slot : PLANES * (slot + 1), 4 * quad : 4 * quad + 4, :].bitcast(F32),
+                )
+
+        def load_scales(load):
+            if load == 1:
+                load_wa_planes(slice(0, A_COLS // 2))
+            elif load == 2:
+                load_wa_planes(slice(A_COLS // 2, A_COLS))
+            elif load in (3, 4, 5, 6):
+                load_wb_planes(load - 3)
+
+        def hold(words, load):
+            if load in (1, 2, 3, 4):
+                nc.gpsimd.memset(words, 0)
+
         wa_tiles = {}
         for first_col in range(0, A_COLS, TILE_COLS):
             width = min(TILE_COLS, A_COLS - first_col)
             wa = weights.tile([P, TILE_PASSES, TILE_COLS], I32, tag="w", align_bytes=64)
+            load = first_col // TILE_COLS
+            load_scales(load)
+            hold(wa[:, 0, 0:HOLD_WORDS], load)
             nc.sync.dma_start(out=wa[:, :, 0:width], in_=wa_words[:, :, first_col : first_col + width])
             wa_tiles[first_col] = wa
         wb_full = []
         for first_pass in range(0, FULL_PASSES, TILE_PASSES):
             wb = weights.tile([P, TILE_PASSES, TILE_COLS], I32, tag="w", align_bytes=64)
+            load = len(wa_tiles) + first_pass // TILE_PASSES
+            load_scales(load)
+            hold(wb[:, 0, 0:HOLD_WORDS], load)
             nc.sync.dma_start(out=wb[:], in_=wb_words[:, first_pass : first_pass + TILE_PASSES, :])
             wb_full.extend([wb[:, i, :] for i in range(TILE_PASSES)])
         wb_split = {}
@@ -87,24 +125,6 @@ def tile_multiheadlatentattention_pb_k_kernel(
                     nc.sync.dma_start(out=words, in_=wb_words[:, g, first_col : first_col + width])
                     wb_split[(part, g)] = words
 
-        ident = keep.tile([P, P], F32)
-        make_identity(nc, ident[:])
-        partition_i = keep.tile([P, 1], I32)
-        nc.gpsimd.iota(partition_i[:], pattern=[[0, 1]], base=0, channel_multiplier=1)
-
-        for col in range(0, A_COLS, A_COLS // 2):
-            cols = slice(col, col + A_COLS // 2)
-            for quad in range(QUADRANTS):
-                nc.gpsimd.dma_start(
-                    out=wa_planes[32 * quad : 32 * quad + 4 * X_PASSES, cols].bitcast(F32),
-                    in_=Wkva_scales[:, 4 * quad : 4 * quad + 4, cols].bitcast(F32),
-                )
-        for slot in range(H_PASSES // PLANES):
-            for quad in range(QUADRANTS):
-                nc.gpsimd.dma_start(
-                    out=wb_planes[32 * quad : 32 * quad + 4 * PLANES, slot, :].bitcast(F32),
-                    in_=Wkvb_scales[PLANES * slot : PLANES * (slot + 1), 4 * quad : 4 * quad + 4, :].bitcast(F32),
-                )
 
         freq = keep.tile([P, DR], F32)
         nc.vector.memset(freq[:, 0:1], 1.0)

@@ -35,6 +35,8 @@ BLOCK = DN
 HEAD_BLOCKS = (DN + DV) // BLOCK
 QUADRANTS = 4
 HOLD_WORDS = 16
+WA_HALF_COLS = RKV // 2
+EARLY_PASSES = 4
 BATCH = 3
 WEIGHT_BUFS = 5
 
@@ -51,7 +53,7 @@ def tile_multiheadlatentattention_pb_k_kernel(
     with tc.tile_pool(name="keep", bufs=1) as keep, tc.tile_pool(name="weights", bufs=WEIGHT_BUFS) as weights, tc.tile_pool(
         name="work", bufs=2
     ) as work, tc.psum_pool(name="psum", bufs=8) as psum, tc.manual_schedule():
-        wa_planes = keep.tile([P, A_COLS], U8, align_bytes=64)
+        wa_planes = keep.tile([P, A_COLS - WA_HALF_COLS], U8, align_bytes=64)
         wb_planes = keep.tile([P, H_PASSES // PLANES, KV_COLS], U8, align_bytes=64)
         gain_rows = keep.tile([P, K_PASS], BF16)
         nc.vector.memset(gain_rows[:].bitcast(I32), 0)
@@ -68,12 +70,14 @@ def tile_multiheadlatentattention_pb_k_kernel(
         partition_i = keep.tile([P, 1], I32)
         nc.gpsimd.iota(partition_i[:], pattern=[[0, 1]], base=0, channel_multiplier=1)
 
-        def load_wa_planes(cols):
-            for quad in range(QUADRANTS):
-                nc.gpsimd.dma_start(
-                    out=wa_planes[32 * quad : 32 * quad + 4 * X_PASSES, cols].bitcast(F32),
-                    in_=Wkva_scales[:, 4 * quad : 4 * quad + 4, cols].bitcast(F32),
-                )
+        def load_wa_planes(quads):
+            for quad in quads:
+                for half, cols in enumerate((slice(0, WA_HALF_COLS), slice(WA_HALF_COLS, A_COLS))):
+                    row = 32 * quad + 4 * X_PASSES * half
+                    nc.gpsimd.dma_start(
+                        out=wa_planes[row : row + 4 * X_PASSES, 0 : cols.stop - cols.start].bitcast(F32),
+                        in_=Wkva_scales[:, 4 * quad : 4 * quad + 4, cols].bitcast(F32),
+                    )
 
         def load_wb_planes(slot):
             for quad in range(QUADRANTS):
@@ -84,9 +88,9 @@ def tile_multiheadlatentattention_pb_k_kernel(
 
         def load_scales(load):
             if load == 1:
-                load_wa_planes(slice(0, A_COLS // 2))
+                load_wa_planes((0, 1))
             elif load == 2:
-                load_wa_planes(slice(A_COLS // 2, A_COLS))
+                load_wa_planes((2, 3))
             elif load in (3, 4, 5, 6):
                 load_wb_planes(load - 3)
 
@@ -104,26 +108,23 @@ def tile_multiheadlatentattention_pb_k_kernel(
             nc.sync.dma_start(out=wa[:, :, 0:width], in_=wa_words[:, :, first_col : first_col + width])
             wa_tiles[first_col] = wa
         wb_full = []
-        for first_pass in range(0, FULL_PASSES, TILE_PASSES):
-            wb = weights.tile([P, TILE_PASSES, TILE_COLS], I32, tag="w", align_bytes=64)
+
+        def load_full(first_pass, start_load):
+            wb = weights.tile([P, TILE_PASSES, TILE_COLS], I32, tag="w", align_bytes=64, name="wb")
             load = len(wa_tiles) + first_pass // TILE_PASSES
             load_scales(load)
             hold(wb[:, 0, 0:HOLD_WORDS], load)
-            nc.sync.dma_start(out=wb[:], in_=wb_words[:, first_pass : first_pass + TILE_PASSES, :])
+            start_load(wb[:], wb_words[:, first_pass : first_pass + TILE_PASSES, :])
             wb_full.extend([wb[:, i, :] for i in range(TILE_PASSES)])
-        wb_split = {}
-        for part in range(2):
-            first_col = PART_FIRST_HEAD[part] * (DN + DV)
-            width = PART_HEADS[part] * (DN + DV)
-            for first_pass in range(FULL_PASSES, H_PASSES, TILE_PASSES):
-                if part == 0 or first_pass == FULL_PASSES:
-                    wb = weights.tile([P, TILE_PASSES * TILE_COLS], I32, tag="w", align_bytes=64)
-                for i in range(TILE_PASSES):
-                    slot = i if part == 0 else first_pass - FULL_PASSES + i
-                    words = wb[:, slot * width : (slot + 1) * width]
-                    g = first_pass + i
-                    nc.sync.dma_start(out=words, in_=wb_words[:, g, first_col : first_col + width])
-                    wb_split[(part, g)] = words
+
+        def load_on_sync(out, in_):
+            nc.sync.dma_start(out=out, in_=in_)
+
+        def load_on_scalar(out, in_):
+            nc.scalar.dma_start(out=out.bitcast(F32), in_=in_.bitcast(F32))
+
+        for first_pass in range(0, EARLY_PASSES, TILE_PASSES):
+            load_full(first_pass, load_on_sync)
 
 
         freq = keep.tile([P, DR], F32)
@@ -191,6 +192,7 @@ def tile_multiheadlatentattention_pb_k_kernel(
             col = bank * BANK
             n = min(BANK, A_COLS - col)
             first_col = col // TILE_COLS * TILE_COLS
+            half = int(col >= WA_HALF_COLS)
             acc = psum.tile([P, BANK], F32, tag="bank", name="acc")
             for g in range(X_PASSES):
                 nc.tensor.matmul_mx(
@@ -198,7 +200,7 @@ def tile_multiheadlatentattention_pb_k_kernel(
                     lhsT=x_codes[:, g, :].bitcast(FP8X4),
                     lhsT_scale=x_planes[:, g, :],
                     rhs=wa_tiles[first_col][:, g, col - first_col : col - first_col + n].bitcast(FP8X4),
-                    rhs_scale=wa_planes[4 * g : P, col : col + n],
+                    rhs_scale=wa_planes[4 * X_PASSES * half + 4 * g : P, col - half * WA_HALF_COLS : col - half * WA_HALF_COLS + n],
                     start=(g == 0),
                     stop=(g == X_PASSES - 1),
                 )
@@ -276,6 +278,23 @@ def tile_multiheadlatentattention_pb_k_kernel(
             )
             k_tiles.append(k_sb)
 
+        for first_pass in range(EARLY_PASSES, FULL_PASSES, TILE_PASSES):
+            load_full(first_pass, load_on_sync if first_pass // TILE_PASSES % 2 == 0 else load_on_scalar)
+        wb_split = {}
+        for part in range(2):
+            first_col = PART_FIRST_HEAD[part] * (DN + DV)
+            width = PART_HEADS[part] * (DN + DV)
+            for first_pass in range(FULL_PASSES, H_PASSES, TILE_PASSES):
+                if part == 0 or first_pass == FULL_PASSES:
+                    wb_part = weights.tile([P, TILE_PASSES * TILE_COLS], I32, tag="w", align_bytes=64)
+                for i in range(TILE_PASSES):
+                    slot = i if part == 0 else first_pass - FULL_PASSES + i
+                    words = wb_part[:, slot * width : (slot + 1) * width]
+                    g = first_pass + i
+                    start_load = load_on_sync if i == 0 else load_on_scalar
+                    start_load(words, wb_words[:, g, first_col : first_col + width])
+                    wb_split[(part, g)] = words
+
         inv_rms = keep.tile([P, 1], F32)
         nc.vector.reciprocal(out=inv_rms[:], in_=rms[:])
         inv_row = psum.tile([P, P], F32, tag="bank")
@@ -350,4 +369,4 @@ def tile_multiheadlatentattention_pb_k_kernel(
             heads = slice(PART_FIRST_HEAD[part], PART_FIRST_HEAD[part] + PART_HEADS[part])
             for b in range(B):
                 nc.sync.dma_start(out=out_0[b, heads, :, :].rearrange("h s f -> s h f"), in_=k_sb[b:P:B, :, :])
-                nc.sync.dma_start(out=out_1[b, heads, :, :].rearrange("h s f -> s h f"), in_=v_sb[b:P:B, :, :])
+                nc.scalar.dma_start(out=out_1[b, heads, :, :].rearrange("h s f -> s h f"), in_=v_sb[b:P:B, :, :])

import math

import concourse.mybir as mybir
from concourse.masks import make_identity

F32 = mybir.dt.float32
BF16 = mybir.dt.bfloat16
I32 = mybir.dt.int32
U32 = mybir.dt.uint32
U8 = mybir.dt.uint8
FP8X4 = mybir.dt.float8_e4m3fn_x4
ALU = mybir.AluOpType
ACT = mybir.ActivationFunctionType

B, S, D, H, DN, DR, DV, RKV = 2, 64, 1024, 16, 64, 128, 128, 8192
THETA = 10000.0
EPS = 1e-6

P = 128
PACK = 4
K_PASS = P * PACK
BANK = 512
X_PASSES = D // K_PASS
H_PASSES = RKV // K_PASS
A_COLS = RKV + DR
KV_COLS = H * (DN + DV)
PART_HEADS = (12, 4)
PART_FIRST_HEAD = (0, 12)
TILE_COLS = KV_COLS
TILE_PASSES = 2
SPLIT_PASSES = 8
FULL_PASSES = H_PASSES - SPLIT_PASSES
PLANES = 4
BLOCK = DN
HEAD_BLOCKS = (DN + DV) // BLOCK
QUADRANTS = 4
HOLD_WORDS = 16
WA_HALF_COLS = RKV // 2
EARLY_PASSES = 4
BATCH = 3
WEIGHT_BUFS = 5

FLOPS = 2 * P * D * A_COLS + 2 * P * RKV * KV_COLS


def tile_multiheadlatentattention_pb_k_kernel(
    tc, x, Wkva_words, Wkva_scales, kv_a_norm_w, Wkvb_words, Wkvb_scales, out_0, out_1
):
    nc = tc.nc
    wa_words = Wkva_words.rearrange("g p n t -> p g (n t)").bitcast(I32)
    wb_words = Wkvb_words.rearrange("g p n t -> p g (n t)").bitcast(I32)

    with tc.tile_pool(name="keep", bufs=1) as keep, tc.tile_pool(name="weights", bufs=WEIGHT_BUFS) as weights, tc.tile_pool(
        name="work", bufs=2
    ) as work, tc.psum_pool(name="psum", bufs=8) as psum, tc.manual_schedule():
        wa_planes = keep.tile([P, A_COLS - WA_HALF_COLS], U8, align_bytes=64)
        wb_planes = keep.tile([P, H_PASSES // PLANES, KV_COLS], U8, align_bytes=64)
        gain_rows = keep.tile([P, K_PASS], BF16)
        nc.vector.memset(gain_rows[:].bitcast(I32), 0)
        nc.vector.memset(wa_planes[:].bitcast(I32), 0)
        nc.vector.memset(wb_planes[:].rearrange("p a n -> p (a n)").bitcast(I32), 0)

        x_sb = keep.tile([P, D], BF16)
        for b in range(B):
            nc.sync.dma_start(out=x_sb[b:P:B, :], in_=x[b])
        nc.sync.dma_start(out=gain_rows[0:H_PASSES, :], in_=kv_a_norm_w.rearrange("(g k) -> g k", k=K_PASS))

        ident = keep.tile([P, P], F32)
        make_identity(nc, ident[:])
        partition_i = keep.tile([P, 1], I32)
        nc.gpsimd.iota(partition_i[:], pattern=[[0, 1]], base=0, channel_multiplier=1)

        def load_wa_planes(quads):
            for quad in quads:
                for half, cols in enumerate((slice(0, WA_HALF_COLS), slice(WA_HALF_COLS, A_COLS))):
                    row = 32 * quad + 4 * X_PASSES * half
                    nc.gpsimd.dma_start(
                        out=wa_planes[row : row + 4 * X_PASSES, 0 : cols.stop - cols.start].bitcast(F32),
                        in_=Wkva_scales[:, 4 * quad : 4 * quad + 4, cols].bitcast(F32),
                    )

        def load_wb_planes(slot):
            for quad in range(QUADRANTS):
                nc.gpsimd.dma_start(
                    out=wb_planes[32 * quad : 32 * quad + 4 * PLANES, slot, :].bitcast(F32),
                    in_=Wkvb_scales[PLANES * slot : PLANES * (slot + 1), 4 * quad : 4 * quad + 4, :].bitcast(F32),
                )

        def load_scales(load):
            if load == 1:
                load_wa_planes((0, 1))
            elif load == 2:
                load_wa_planes((2, 3))
            elif load in (3, 4, 5, 6):
                load_wb_planes(load - 3)

        def hold(words, load):
            if load in (1, 2, 3, 4):
                nc.gpsimd.memset(words, 0)

        wa_tiles = {}
        for first_col in range(0, A_COLS, TILE_COLS):
            width = min(TILE_COLS, A_COLS - first_col)
            wa = weights.tile([P, TILE_PASSES, TILE_COLS], I32, tag="w", align_bytes=64)
            load = first_col // TILE_COLS
            load_scales(load)
            hold(wa[:, 0, 0:HOLD_WORDS], load)
            nc.sync.dma_start(out=wa[:, :, 0:width], in_=wa_words[:, :, first_col : first_col + width])
            wa_tiles[first_col] = wa
        wb_full = []

        def load_full(first_pass, start_load):
            wb = weights.tile([P, TILE_PASSES, TILE_COLS], I32, tag="w", align_bytes=64, name="wb")
            load = len(wa_tiles) + first_pass // TILE_PASSES
            load_scales(load)
            hold(wb[:, 0, 0:HOLD_WORDS], load)
            start_load(wb[:], wb_words[:, first_pass : first_pass + TILE_PASSES, :])
            wb_full.extend([wb[:, i, :] for i in range(TILE_PASSES)])

        def load_on_sync(out, in_):
            nc.sync.dma_start(out=out, in_=in_)

        def load_on_scalar(out, in_):
            nc.scalar.dma_start(out=out.bitcast(F32), in_=in_.bitcast(F32))

        for first_pass in range(0, EARLY_PASSES, TILE_PASSES):
            load_full(first_pass, load_on_sync)


        freq = keep.tile([P, DR], F32)
        nc.vector.memset(freq[:, 0:1], 1.0)
        for i in range(6):
            step = 2**i
            nc.vector.tensor_single_scalar(
                out=freq[:, step : 2 * step], in_=freq[:, 0:step], scalar=THETA ** (-step / 64.0), op=ALU.mult
            )
        nc.vector.tensor_copy(out=freq[:, 64:128], in_=freq[:, 0:64])
        position_i = keep.tile([P, 1], I32)
        nc.vector.tensor_single_scalar(out=position_i[:], in_=partition_i[:], scalar=1, op=ALU.arith_shift_right)
        position_turns = keep.tile([P, 1], F32)
        nc.vector.tensor_single_scalar(out=position_turns[:], in_=position_i[:], scalar=1.0 / (2.0 * math.pi), op=ALU.mult)
        turns = keep.tile([P, 2, DR], F32)
        for c in range(2):
            nc.vector.tensor_scalar(
                out=turns[:, c, :], in0=freq[:], scalar1=position_turns[:, 0:1], scalar2=0.25 * c, op0=ALU.mult, op1=ALU.add
            )
        turns_flat = turns[:].rearrange("p c j -> p (c j)")
        whole_i = keep.tile([P, 2 * DR], I32)
        nc.vector.tensor_copy(out=whole_i[:], in_=turns_flat)
        whole = keep.tile([P, 2 * DR], F32)
        nc.vector.tensor_copy(out=whole[:], in_=whole_i[:])
        frac = turns_flat
        nc.vector.tensor_tensor(out=frac, in0=turns_flat, in1=whole[:], op=ALU.subtract)
        minus_frac = whole
        nc.vector.scalar_tensor_tensor(
            out=minus_frac[:], in0=frac, scalar=0.5, in1=frac, op0=ALU.is_gt, op1=ALU.subtract
        )
        sin_cos = keep.tile([P, 2, DR // 2, 2], F32)
        nc.scalar.activation(
            out=sin_cos[:].rearrange("p c i e -> p (c i e)"), in_=minus_frac[:], func=ACT.Sin, scale=-2.0 * math.pi
        )
        first_sqrt = keep.tile([P, 1], F32)
        nc.scalar.sqrt(out=first_sqrt[:], in_=freq[:, 0:1])

        x_words = x_sb[:].bitcast(F32)
        xt = psum.tile([P, X_PASSES, 2, P], F32, tag="bank")
        for g in range(X_PASSES):
            for u in range(2):
                nc.tensor.transpose(xt[:, g, u, :], x_words[:, (K_PASS // 2) * g + u : (K_PASS // 2) * (g + 1) : 2], ident[:])
        x_grouped = keep.tile([P, X_PASSES, P, PACK], BF16, align_bytes=64)
        nc.vector.tensor_copy(out=x_grouped[:].bitcast(F32), in_=xt[:].rearrange("p g u m -> p g m u"))
        x_codes = keep.tile([P, X_PASSES, P], U32, align_bytes=64)
        x_planes = keep.tile([P, X_PASSES, P], U8, align_bytes=64)
        nc.vector.quantize_mx(
            out=x_codes[:].rearrange("p g m -> p (g m)").bitcast(FP8X4),
            scales=x_planes[:].rearrange("p g m -> p (g m)"),
            in_=x_grouped[:].rearrange("p g m t -> p (g m t)"),
        )

        gain_words = gain_rows[:].bitcast(F32)
        gt = psum.tile([P, 2, P], F32, tag="bank")
        for u in range(2):
            nc.tensor.transpose(gt[:, u, :], gain_words[:, u : K_PASS // 2 : 2], ident[:])
        gain_kt = keep.tile([P, H_PASSES, PACK], BF16)
        nc.vector.tensor_copy(out=gain_kt[:].bitcast(F32), in_=gt[:, :, 0:H_PASSES].rearrange("p u g -> p g u"))

        c_gain = keep.tile([P, H_PASSES, P, PACK], F32)
        sum_squares = keep.tile([P, H_PASSES], F32)
        c_tiles = {}

        def multiply_a(bank):
            col = bank * BANK
            n = min(BANK, A_COLS - col)
            first_col = col // TILE_COLS * TILE_COLS
            half = int(col >= WA_HALF_COLS)
            acc = psum.tile([P, BANK], F32, tag="bank", name="acc")
            for g in range(X_PASSES):
                nc.tensor.matmul_mx(
                    out=acc[:, 0:n],
                    lhsT=x_codes[:, g, :].bitcast(FP8X4),
                    lhsT_scale=x_planes[:, g, :],
                    rhs=wa_tiles[first_col][:, g, col - first_col : col - first_col + n].bitcast(FP8X4),
                    rhs_scale=wa_planes[4 * X_PASSES * half + 4 * g : P, col - half * WA_HALF_COLS : col - half * WA_HALF_COLS + n],
                    start=(g == 0),
                    stop=(g == X_PASSES - 1),
                )
            return acc

        def copy_c(bank, acc, copy):
            c_tiles[bank] = work.tile([P, PACK, P], F32, tag="c", bufs=2 * BATCH, name="c_tile")
            copy(out=c_tiles[bank][:], in_=acc[:].rearrange("m (p t) -> m t p", t=PACK))

        def add_squares(bank):
            squares = work.tile([P, PACK, P], BF16)
            nc.scalar.activation(
                out=squares[:], in_=c_tiles[bank][:], func=ACT.Square, accum_out=sum_squares[:, bank : bank + 1]
            )

        def transpose_c(bank):
            ct = psum.tile([P, PACK, P], F32, tag="bank", name="ct")
            for t in range(PACK):
                nc.tensor.transpose(ct[:, t, :], c_tiles[bank][:, t, :], ident[:])
            return ct

        def apply_gain(bank, ct):
            nc.vector.tensor_tensor(
                out=c_gain[:, bank, :, :],
                in0=ct[:].rearrange("p t m -> p m t"),
                in1=gain_kt[:, bank, :].unsqueeze(1).to_broadcast([P, P, PACK]),
                op=ALU.mult,
            )

        before = []
        for first_bank in range(0, H_PASSES, BATCH):
            banks = list(range(first_bank, min(first_bank + BATCH, H_PASSES)))
            accs = [multiply_a(bank) for bank in banks]
            if banks[-1] == H_PASSES - 1:
                r_acc = multiply_a(H_PASSES)
            cts = [transpose_c(bank) for bank in before]
            for bank, acc in zip(banks, accs):
                copy_c(bank, acc, nc.vector.tensor_copy if bank == first_bank else nc.scalar.copy)
            for bank in banks:
                add_squares(bank)
            for bank, ct in zip(before, cts):
                apply_gain(bank, ct)
            before = banks
        for bank in before:
            apply_gain(bank, transpose_c(bank))

        others = keep.tile([P, 1], F32)
        nc.vector.reduce_sum(out=others[:], in_=sum_squares[:, 0 : H_PASSES - 1], axis=mybir.AxisListType.X)
        others_mean = keep.tile([P, 1], F32)
        nc.vector.tensor_scalar(
            out=others_mean[:], in0=others[:], scalar1=1.0 / RKV, scalar2=EPS, op0=ALU.mult, op1=ALU.add
        )
        rms = keep.tile([P, 1], F32)
        nc.scalar.activation(
            out=rms[:], in_=sum_squares[:, H_PASSES - 1 : H_PASSES], func=ACT.Sqrt, scale=1.0 / RKV, bias=others_mean[:, 0:1]
        )

        rope = keep.tile([P, DR // 2, 2], F32)
        r = r_acc[:, 0:DR].rearrange("m (i e) -> m i e", e=2)
        r_cos = keep.tile([P, DR // 2, 2], F32)
        r_sin = keep.tile([P, DR // 2, 2], F32)
        nc.vector.tensor_tensor(out=r_cos[:], in0=r, in1=sin_cos[:, 1, :, :], op=ALU.mult)
        for e in range(2):
            nc.vector.tensor_tensor(
                out=r_sin[:, :, e : e + 1], in0=r[:, :, 1 - e : 2 - e], in1=sin_cos[:, 0, :, e : e + 1], op=ALU.mult
            )
        nc.vector.tensor_tensor(out=rope[:, :, 0:1], in0=r_cos[:, :, 0:1], in1=r_sin[:, :, 0:1], op=ALU.subtract)
        nc.vector.tensor_tensor(out=rope[:, :, 1:2], in0=r_cos[:, :, 1:2], in1=r_sin[:, :, 1:2], op=ALU.add)
        k_tiles = []
        for heads in PART_HEADS:
            k_sb = keep.tile([P, heads, DN + DR], F32, name="k_sb%d" % len(k_tiles))
            nc.vector.tensor_copy(
                out=k_sb[:, :, DN : DN + DR],
                in_=rope[:].rearrange("m i e -> m (i e)").unsqueeze(1).to_broadcast([P, heads, DR]),
            )
            k_tiles.append(k_sb)

        for first_pass in range(EARLY_PASSES, FULL_PASSES, TILE_PASSES):
            load_full(first_pass, load_on_sync if first_pass // TILE_PASSES % 2 == 0 else load_on_scalar)
        wb_split = {}
        for part in range(2):
            first_col = PART_FIRST_HEAD[part] * (DN + DV)
            width = PART_HEADS[part] * (DN + DV)
            for first_pass in range(FULL_PASSES, H_PASSES, TILE_PASSES):
                if part == 0 or first_pass == FULL_PASSES:
                    wb_part = weights.tile([P, TILE_PASSES * TILE_COLS], I32, tag="w", align_bytes=64)
                for i in range(TILE_PASSES):
                    slot = i if part == 0 else first_pass - FULL_PASSES + i
                    words = wb_part[:, slot * width : (slot + 1) * width]
                    g = first_pass + i
                    start_load = load_on_sync if i == 0 else load_on_scalar
                    start_load(words, wb_words[:, g, first_col : first_col + width])
                    wb_split[(part, g)] = words

        inv_rms = keep.tile([P, 1], F32)
        nc.vector.reciprocal(out=inv_rms[:], in_=rms[:])
        inv_row = psum.tile([P, P], F32, tag="bank")
        nc.tensor.transpose(inv_row[:], inv_rms[:, 0:1].to_broadcast([P, P]), ident[:])

        h_codes = keep.tile([P, H_PASSES, P], U32, align_bytes=64)
        h_planes = keep.tile([P, H_PASSES, P], U8, align_bytes=64)
        h_tiles = {}

        def scale_h(g):
            h_tiles[g] = work.tile([P, P, PACK], BF16, tag="h", bufs=3, align_bytes=64, name="h_tile")
            nc.vector.tensor_tensor(
                out=h_tiles[g][:],
                in0=c_gain[:, g, :, :],
                in1=inv_row[:].unsqueeze(2).to_broadcast([P, P, PACK]),
                op=ALU.mult,
            )

        def quantize_h(g):
            nc.vector.quantize_mx(
                out=h_codes[:, g, :].bitcast(FP8X4),
                scales=h_planes[:, g, :],
                in_=h_tiles[g][:].rearrange("p m t -> p (m t)"),
            )

        scale_h(0)
        for g in range(1, H_PASSES):
            scale_h(g)
            quantize_h(g - 1)
        quantize_h(H_PASSES - 1)

        chunks = []
        for part in range(2):
            width = PART_HEADS[part] * (DN + DV)
            chunks.append(
                [(at, min(BANK, width - at), psum.tile([P, BANK], F32, tag="bank", name="kv_acc")) for at in range(0, width, BANK)]
            )

        def multiply(g, part, words, offset):
            first_col = PART_FIRST_HEAD[part] * (DN + DV)
            for at, n, acc in chunks[part]:
                nc.tensor.matmul_mx(
                    out=acc[:, 0:n],
                    lhsT=h_codes[:, g, :].bitcast(FP8X4),
                    lhsT_scale=h_planes[:, g, :],
                    rhs=words[:, offset + at : offset + at + n].bitcast(FP8X4),
                    rhs_scale=wb_planes[4 * (g % PLANES) : P, g // PLANES, first_col + at : first_col + at + n],
                    start=(g == 0),
                    stop=(g == H_PASSES - 1),
                )

        for g in range(FULL_PASSES):
            for part in range(2):
                multiply(g, part, wb_full[g], PART_FIRST_HEAD[part] * (DN + DV))
        for part in range(2):
            for g in range(FULL_PASSES, H_PASSES):
                multiply(g, part, wb_split[(part, g)], 0)
            k_sb = k_tiles[part]
            v_sb = work.tile([P, PART_HEADS[part], DV], F32, tag="v%d" % part, bufs=1, name="v_sb")
            for i, (at, n, acc) in enumerate(chunks[part]):
                copy = nc.vector.tensor_copy if i % 2 == 0 else nc.scalar.copy
                blocks = acc[:, 0:n].rearrange("m (j f) -> m j f", f=BLOCK)
                for kind in range(HEAD_BLOCKS):
                    first = (kind - at // BLOCK) % HEAD_BLOCKS
                    found = blocks[:, first : n // BLOCK : HEAD_BLOCKS, :]
                    head = (at // BLOCK + first) // HEAD_BLOCKS
                    heads = slice(head, head + found.shape[1])
                    if kind == 0:
                        copy(out=k_sb[:, heads, 0:DN], in_=found)
                    else:
                        copy(out=v_sb[:, heads, (kind - 1) * BLOCK : kind * BLOCK], in_=found)
            heads = slice(PART_FIRST_HEAD[part], PART_FIRST_HEAD[part] + PART_HEADS[part])
            for b in range(B):
                nc.sync.dma_start(out=out_0[b, heads, :, :].rearrange("h s f -> s h f"), in_=k_sb[b:P:B, :, :])
                nc.scalar.dma_start(out=out_1[b, heads, :, :].rearrange("h s f -> s h f"), in_=v_sb[b:P:B, :, :])
